import numpy as np
import ml_dtypes


def mxq(x, axis, fmt="e4m3"):
    dtype, down = {"e4m3": (ml_dtypes.float8_e4m3fn, 7), "e5m2": (ml_dtypes.float8_e5m2, 14)}[fmt]
    v = np.moveaxis(np.asarray(x, np.float32).astype(ml_dtypes.bfloat16).astype(np.float64), axis, -1)
    blocks = v.reshape(v.shape[:-1] + (-1, 32))
    amax = np.abs(blocks).max(-1, keepdims=True)
    byte = np.maximum(np.where(amax > 0, np.frexp(amax)[1] - 1 + 127, 0) - down, 1)
    scale = np.exp2(byte - 127.0)
    codes = (blocks / scale).astype(np.float32).astype(dtype).astype(np.float64)
    return np.moveaxis((codes * scale).reshape(v.shape), -1, axis)


WIDE = False


def mx_kscale(k):
    if not WIDE:
        return np.ones(k)
    levels = np.array([10, -10, 5, -5, 0])
    if k % 512:
        return np.exp2(np.random.permutation(np.resize(levels, k // 32))).repeat(32)
    a = np.empty((k // 512, 16))
    for p in range(k // 512):
        a[p, :8] = np.random.permutation(np.resize(levels, 8))
        for g in range(8):
            far = levels[np.abs(levels - a[p, g]) >= 10]
            a[p, g + 8] = far[np.random.randint(len(far))]
    return np.exp2(a.ravel()).repeat(32)


BF16 = ml_dtypes.bfloat16


def bf(x):
    return np.asarray(x, np.float32).astype(BF16)


def f64(x):
    return np.asarray(x).astype(np.float64)


B, IN_F, OUT_F = 512, 16384, 512
EPS = 1e-5


def setup_inputs():
    s = mx_kscale(IN_F)
    scale = 1.0 / np.sqrt(IN_F)
    return {"x": bf(np.random.standard_normal((B, IN_F)) * s),
            "y": bf(np.random.standard_normal((B, OUT_F))),
            "weight": bf(np.random.uniform(-scale, scale, (OUT_F, IN_F)) / s[None, :]),
            "bias": bf(np.random.uniform(-0.5, 0.5, OUT_F)),
            "running_mean": bf(np.random.standard_normal(OUT_F) * 0.3),
            "running_var": bf(np.random.uniform(0.5, 1.5, OUT_F)),
            "norm_weight": bf(1.0 + 0.1 * np.random.standard_normal(OUT_F)),
            "norm_bias": bf(np.random.standard_normal(OUT_F) * 0.3)}


def reference(x, y, weight, bias, running_mean, running_var, norm_weight, norm_bias):
    linear = (mxq(f64(x), 1, "e4m3") @ mxq(f64(weight), 1, "e4m3").T) + f64(bias)
    inv_std = 1.0 / np.sqrt(f64(running_var) + EPS)
    norm = (linear - f64(running_mean)) * inv_std * f64(norm_weight) + f64(norm_bias)
    return (norm + f64(y)) * f64(y)

@@ -1,0 +1,220 @@
+from contextlib import ExitStack
+
+import concourse.mybir as mybir
+from concourse.masks import make_identity
+
+F32 = mybir.dt.float32
+BF16 = mybir.dt.bfloat16
+U32 = mybir.dt.uint32
+U8 = mybir.dt.uint8
+FP8X4 = mybir.dt.float8_e4m3fn_x4
+SQRT = mybir.ActivationFunctionType.Sqrt
+
+P = 128
+PACK = 4
+K_PASS = P * PACK
+BANK = 512
+
+ROWS = 512
+FEATURES = 512
+K = 16384
+EPS = 1e-5
+BLOCKS = ROWS // P
+PASSES = K // K_PASS
+WORDS = K_PASS // 2
+PER_PARTITION = FEATURES // P
+
+CHUNK_MAX = 1024
+PREFETCH = 6
+ROUND_PASSES = 2
+ROUNDS = PASSES // ROUND_PASSES
+LAG = 1
+PASS_BANKS = 4
+VECTOR_BANK = 2
+
+FLOPS = 2 * ROWS * FEATURES * K
+
+
+def chunk_widths():
+    widths = [K_PASS]
+    while sum(widths) < K:
+        widths.append(min(sum(widths), CHUNK_MAX))
+    assert sum(widths) == K
+    return widths
+
+
+def tile_modelnew_k_kernel(
+    tc, x, y, weight, bias, running_mean, running_var, norm_weight, norm_bias, out
+):
+    nc = tc.nc
+    widths = chunk_widths()
+    home = [(c, i) for c, width in enumerate(widths) for i in range(width // K_PASS)]
+    x_view = x.rearrange("(b p) k -> p b k", p=P)
+    w_view = weight.rearrange("(b p) k -> p b k", p=P)
+    y_view = y.rearrange("(b p) n -> p b n", p=P)
+
+    with ExitStack() as ctx:
+        consts = ctx.enter_context(tc.tile_pool(name="consts", bufs=1))
+        stage = ctx.enter_context(tc.tile_pool(name="stage", bufs=PREFETCH))
+        group_pool = ctx.enter_context(tc.tile_pool(name="grouped", bufs=2 * ROUND_PASSES))
+        code_pool = ctx.enter_context(tc.tile_pool(name="codes", bufs=(LAG + 1) * ROUND_PASSES))
+        result_pool = ctx.enter_context(tc.tile_pool(name="result", bufs=BLOCKS))
+        turn_psum = ctx.enter_context(tc.psum_pool(name="turn", bufs=PASS_BANKS))
+        acc_psum = ctx.enter_context(tc.psum_pool(name="acc", bufs=1))
+        ctx.enter_context(tc.manual_schedule())
+
+        staged = {}
+        grouped = {}
+        quantised = {}
+
+        def load_chunk(c):
+            k0, width = sum(widths[:c]), widths[c]
+            x_st = stage.tile([P, BLOCKS * width], BF16, tag="x_st")
+            nc.sync.dma_start(
+                out=x_st[:].rearrange("p (b k) -> p b k", b=BLOCKS),
+                in_=x_view[:, :, k0 : k0 + width],
+            )
+            w_st = stage.tile([P, BLOCKS * width], BF16, tag="w_st")
+            nc.sync.dma_start(
+                out=w_st[:].rearrange("p (b k) -> p b k", b=BLOCKS),
+                in_=w_view[:, :, k0 : k0 + width],
+            )
+            staged[c] = (x_st, w_st)
+
+        def load_vector(vector, name):
+            column = consts.tile([P, PER_PARTITION], BF16, name=name)
+            nc.scalar.dma_start(out=column[:], in_=vector.rearrange("(p j) -> p j", j=PER_PARTITION))
+            return column
+
+        var_col = load_vector(running_var, "var_col")
+        gain_col = load_vector(norm_weight, "gain_col")
+        bias_col = load_vector(bias, "bias_col")
+        mean_col = load_vector(running_mean, "mean_col")
+        offset_col = load_vector(norm_bias, "offset_col")
+
+        for c in range(PREFETCH):
+            load_chunk(c)
+        y_sb = consts.tile([P, BLOCKS * FEATURES], BF16)
+        nc.sync.dma_start(out=y_sb[:].rearrange("p (b n) -> p b n", b=BLOCKS), in_=y_view)
+
+        ident = consts.tile([P, P], F32)
+        make_identity(nc, ident[:])
+
+        scale_col = consts.tile([P, PER_PARTITION], F32)
+        shift_col = consts.tile([P, PER_PARTITION], F32)
+        nc.scalar.activation(out=scale_col[:], in_=var_col[:], func=SQRT, bias=EPS)
+        nc.vector.reciprocal(out=scale_col[:], in_=scale_col[:])
+        nc.vector.tensor_mul(out=scale_col[:], in0=scale_col[:], in1=gain_col[:])
+        nc.vector.tensor_sub(out=shift_col[:], in0=bias_col[:], in1=mean_col[:])
+        nc.vector.tensor_mul(out=shift_col[:], in0=shift_col[:], in1=scale_col[:])
+        nc.vector.tensor_add(out=shift_col[:], in0=shift_col[:], in1=offset_col[:])
+
+        scale_bc = consts.tile([P, FEATURES], F32)
+        shift_bc = consts.tile([P, FEATURES], F32)
+
+        def spread_over_partitions(column, tag):
+            bank = acc_psum.tile([P, BANK], F32, tag=tag, name="spread")
+            for j in range(PER_PARTITION):
+                nc.tensor.transpose(
+                    bank[:, j * P : (j + 1) * P], column[:, j : j + 1].to_broadcast([P, P]), ident[:]
+                )
+            return bank[:].rearrange("m (j p) -> m p j", j=PER_PARTITION)
+
+        factor = consts.tile([P, BLOCKS * FEATURES], F32)
+        addend = consts.tile([P, BLOCKS * FEATURES], F32)
+
+        def prepare_row_block(b):
+            cols = slice(b * FEATURES, (b + 1) * FEATURES)
+            nc.vector.tensor_mul(out=factor[:, cols], in0=scale_bc[:], in1=y_sb[:, cols])
+            nc.vector.tensor_add(out=addend[:, cols], in0=shift_bc[:], in1=y_sb[:, cols])
+            nc.vector.tensor_mul(out=addend[:, cols], in0=addend[:, cols], in1=y_sb[:, cols])
+
+        first_free = sum(widths[:PREFETCH]) // (K_PASS * ROUND_PASSES)
+        prepare_in_round = {first_free + 2 * b: b for b in range(BLOCKS)}
+
+        def transpose_bank(g, j):
+            c, i = home[g]
+            words = staged[c][j // 2][:].bitcast(F32)
+            words_per_block = widths[c] // 2
+            bank = turn_psum.tile([P, BANK], F32, tag="bank")
+            for h in range(2):
+                for u in range(2):
+                    w0 = (2 * (j % 2) + h) * words_per_block + i * WORDS + u
+                    q = 2 * h + u
+                    nc.tensor.transpose(bank[:, q * P : (q + 1) * P], words[:, w0 : w0 + WORDS - u : 2], ident[:])
+            return bank
+
+        def empty_bank(copy, g, j, bank):
+            copy(
+                out=grouped[g][:]
+                .bitcast(F32)[:, j * BANK : (j + 1) * BANK]
+                .rearrange("p (h r u) -> p h r u", h=2, u=2),
+                in_=bank[:].rearrange("p (h u r) -> p h r u", h=2, u=2),
+            )
+
+        def quantise_pass(g):
+            words = code_pool.tile([P, ROWS + FEATURES], U32, align_bytes=64, tag="words")
+            scales = code_pool.tile([P, ROWS + FEATURES], U8, align_bytes=64, tag="scales")
+            nc.vector.quantize_mx(out=words[:].bitcast(FP8X4), scales=scales[:], in_=grouped[g][:])
+            quantised[g] = (words, scales)
+
+        acc = []
+
+        def multiply_pass(g):
+            words, scales = quantised[g]
+            for b in range(BLOCKS):
+                nc.tensor.matmul_mx(
+                    out=acc[b][:],
+                    lhsT=words[:, b * P : (b + 1) * P].bitcast(FP8X4),
+                    lhsT_scale=scales[:, b * P : (b + 1) * P],
+                    rhs=words[:, ROWS : ROWS + FEATURES].bitcast(FP8X4),
+                    rhs_scale=scales[:, ROWS : ROWS + FEATURES],
+                    start=(g == 0),
+                    stop=(g == PASSES - 1),
+                )
+
+        for r in range(ROUNDS):
+            for g in range(r * ROUND_PASSES, (r + 1) * ROUND_PASSES):
+                grouped[g] = group_pool.tile(
+                    [P, (ROWS + FEATURES) * PACK], BF16, align_bytes=64, tag="grouped", name="grouped"
+                )
+                banks = [transpose_bank(g, j) for j in range(PASS_BANKS)]
+                for j in range(PASS_BANKS):
+                    if j != VECTOR_BANK:
+                        empty_bank(nc.scalar.copy, g, j, banks[j])
+                if r >= 1:
+                    quantise_pass(g - ROUND_PASSES)
+                empty_bank(nc.vector.tensor_copy, g, VECTOR_BANK, banks[VECTOR_BANK])
+                c, i = home[g]
+                if (i + 1) * K_PASS == widths[c] and c + PREFETCH < len(widths):
+                    load_chunk(c + PREFETCH)
+
+            if r == LAG - 1:
+                nc.scalar.copy(
+                    out=scale_bc[:].rearrange("m (p j) -> m p j", j=PER_PARTITION),
+                    in_=spread_over_partitions(scale_col, "acc0"),
+                )
+                nc.vector.tensor_copy(
+                    out=shift_bc[:].rearrange("m (p j) -> m p j", j=PER_PARTITION),
+                    in_=spread_over_partitions(shift_col, "acc1"),
+                )
+                for b in range(BLOCKS):
+                    acc.append(acc_psum.tile([P, FEATURES], F32, tag="acc%d" % b, name="acc%d" % b))
+            if r in prepare_in_round:
+                prepare_row_block(prepare_in_round[r])
+
+            if r >= LAG:
+                for g in range((r - LAG) * ROUND_PASSES, (r - LAG + 1) * ROUND_PASSES):
+                    multiply_pass(g)
+
+        for g in range(PASSES - ROUND_PASSES, PASSES):
+            quantise_pass(g)
+        for g in range(PASSES - LAG * ROUND_PASSES, PASSES):
+            multiply_pass(g)
+
+        for b in range(BLOCKS):
+            cols = slice(b * FEATURES, (b + 1) * FEATURES)
+            result = result_pool.tile([P, FEATURES], F32)
+            nc.vector.tensor_mul(out=result[:], in0=acc[b][:], in1=factor[:, cols])
+            nc.vector.tensor_add(out=result[:], in0=result[:], in1=addend[:, cols])
+            nc.sync.dma_start(out=out[b * P : (b + 1) * P, :], in_=result[:])

@@ -25,12 +25,12 @@ WORDS = K_PASS // 2
 PER_PARTITION = FEATURES // P
 
 CHUNK_MAX = 1024
-PREFETCH = 6
+PREFETCH = 5
 ROUND_PASSES = 2
 ROUNDS = PASSES // ROUND_PASSES
 LAG = 1
 PASS_BANKS = 4
-VECTOR_BANK = 2
+HALF = 16
 
 FLOPS = 2 * ROWS * FEATURES * K
 
@@ -56,6 +56,7 @@ def tile_modelnew_k_kernel(
     with ExitStack() as ctx:
         consts = ctx.enter_context(tc.tile_pool(name="consts", bufs=1))
         stage = ctx.enter_context(tc.tile_pool(name="stage", bufs=PREFETCH))
+        order_pool = ctx.enter_context(tc.tile_pool(name="ordered", bufs=3))
         group_pool = ctx.enter_context(tc.tile_pool(name="grouped", bufs=2 * ROUND_PASSES))
         code_pool = ctx.enter_context(tc.tile_pool(name="codes", bufs=(LAG + 1) * ROUND_PASSES))
         result_pool = ctx.enter_context(tc.tile_pool(name="result", bufs=BLOCKS))
@@ -64,6 +65,7 @@ def tile_modelnew_k_kernel(
         ctx.enter_context(tc.manual_schedule())
 
         staged = {}
+        ordered = {}
         grouped = {}
         quantised = {}
 
@@ -132,20 +134,28 @@ def tile_modelnew_k_kernel(
         first_free = sum(widths[:PREFETCH]) // (K_PASS * ROUND_PASSES)
         prepare_in_round = {first_free + 2 * b: b for b in range(BLOCKS)}
 
+        def order_words(c, operand):
+            tile = order_pool.tile([P, BLOCKS * widths[c]], BF16, tag="ordered%d" % operand, name="ordered")
+            source = staged[c][operand][:].rearrange("p (m q u e) -> p u m q e", q=P // 8, u=2, e=HALF)
+            target = tile[:].rearrange("p (u m q e) -> p u m q e", u=2, q=P // 8, e=HALF)
+            for u in range(2):
+                nc.vector.tensor_copy(out=target[:, u], in_=source[:, u])
+            ordered.setdefault(c, []).append(tile)
+
         def transpose_bank(g, j):
             c, i = home[g]
-            words = staged[c][j // 2][:].bitcast(F32)
-            words_per_block = widths[c] // 2
+            words = ordered[c][j // 2][:].bitcast(F32)
+            passes = widths[c] // K_PASS
             bank = turn_psum.tile([P, BANK], F32, tag="bank")
             for h in range(2):
                 for u in range(2):
-                    w0 = (2 * (j % 2) + h) * words_per_block + i * WORDS + u
+                    w0 = ((u * BLOCKS + 2 * (j % 2) + h) * passes + i) * P
                     q = 2 * h + u
-                    nc.tensor.transpose(bank[:, q * P : (q + 1) * P], words[:, w0 : w0 + WORDS - u : 2], ident[:])
+                    nc.tensor.transpose(bank[:, q * P : (q + 1) * P], words[:, w0 : w0 + P], ident[:])
             return bank
 
-        def empty_bank(copy, g, j, bank):
-            copy(
+        def empty_bank(g, j, bank):
+            nc.scalar.copy(
                 out=grouped[g][:]
                 .bitcast(F32)[:, j * BANK : (j + 1) * BANK]
                 .rearrange("p (h r u) -> p h r u", h=2, u=2),
@@ -173,21 +183,28 @@ def tile_modelnew_k_kernel(
                     stop=(g == PASSES - 1),
                 )
 
+        def chunks_of(r):
+            return sorted({home[g][0] for g in range(r * ROUND_PASSES, (r + 1) * ROUND_PASSES)})
+
+        def order_round(r):
+            for c in chunks_of(r):
+                for operand in range(2):
+                    order_words(c, operand)
+                if c + PREFETCH < len(widths):
+                    load_chunk(c + PREFETCH)
+
+        order_round(0)
         for r in range(ROUNDS):
             for g in range(r * ROUND_PASSES, (r + 1) * ROUND_PASSES):
                 grouped[g] = group_pool.tile(
                     [P, (ROWS + FEATURES) * PACK], BF16, align_bytes=64, tag="grouped", name="grouped"
                 )
-                banks = [transpose_bank(g, j) for j in range(PASS_BANKS)]
                 for j in range(PASS_BANKS):
-                    if j != VECTOR_BANK:
-                        empty_bank(nc.scalar.copy, g, j, banks[j])
+                    empty_bank(g, j, transpose_bank(g, j))
                 if r >= 1:
                     quantise_pass(g - ROUND_PASSES)
-                empty_bank(nc.vector.tensor_copy, g, VECTOR_BANK, banks[VECTOR_BANK])
-                c, i = home[g]
-                if (i + 1) * K_PASS == widths[c] and c + PREFETCH < len(widths):
-                    load_chunk(c + PREFETCH)
+            if r + 1 < ROUNDS:
+                order_round(r + 1)
 
             if r == LAG - 1:
                 nc.scalar.copy(

@@ -26,9 +26,7 @@ PER_PARTITION = FEATURES // P
 
 CHUNK_MAX = 1024
 PREFETCH = 5
-ROUND_PASSES = 2
-ROUNDS = PASSES // ROUND_PASSES
-LAG = 1
+LAG = 2
 PASS_BANKS = 4
 HALF = 16
 
@@ -57,8 +55,8 @@ def tile_modelnew_k_kernel(
         consts = ctx.enter_context(tc.tile_pool(name="consts", bufs=1))
         stage = ctx.enter_context(tc.tile_pool(name="stage", bufs=PREFETCH))
         order_pool = ctx.enter_context(tc.tile_pool(name="ordered", bufs=3))
-        group_pool = ctx.enter_context(tc.tile_pool(name="grouped", bufs=2 * ROUND_PASSES))
-        code_pool = ctx.enter_context(tc.tile_pool(name="codes", bufs=(LAG + 1) * ROUND_PASSES))
+        group_pool = ctx.enter_context(tc.tile_pool(name="grouped", bufs=3))
+        code_pool = ctx.enter_context(tc.tile_pool(name="codes", bufs=LAG + 2))
         result_pool = ctx.enter_context(tc.tile_pool(name="result", bufs=BLOCKS))
         turn_psum = ctx.enter_context(tc.psum_pool(name="turn", bufs=PASS_BANKS))
         acc_psum = ctx.enter_context(tc.psum_pool(name="acc", bufs=1))
@@ -131,8 +129,8 @@ def tile_modelnew_k_kernel(
             nc.vector.tensor_add(out=addend[:, cols], in0=shift_bc[:], in1=y_sb[:, cols])
             nc.vector.tensor_mul(out=addend[:, cols], in0=addend[:, cols], in1=y_sb[:, cols])
 
-        first_free = sum(widths[:PREFETCH]) // (K_PASS * ROUND_PASSES)
-        prepare_in_round = {first_free + 2 * b: b for b in range(BLOCKS)}
+        first_free = sum(widths[:PREFETCH]) // K_PASS
+        prepare_after_pass = {first_free + 4 * b: b for b in range(BLOCKS)}
 
         def order_words(c, operand):
             tile = order_pool.tile([P, BLOCKS * widths[c]], BF16, tag="ordered%d" % operand, name="ordered")
@@ -183,30 +181,29 @@ def tile_modelnew_k_kernel(
                     stop=(g == PASSES - 1),
                 )
 
-        def chunks_of(r):
-            return sorted({home[g][0] for g in range(r * ROUND_PASSES, (r + 1) * ROUND_PASSES)})
+        def order_chunk(c, operand):
+            order_words(c, operand)
+            if operand == 1 and c + PREFETCH < len(widths):
+                load_chunk(c + PREFETCH)
 
-        def order_round(r):
-            for c in chunks_of(r):
+        order_chunk(0, 0)
+        order_chunk(0, 1)
+        for g in range(PASSES):
+            grouped[g] = group_pool.tile(
+                [P, (ROWS + FEATURES) * PACK], BF16, align_bytes=64, tag="grouped", name="grouped"
+            )
+            for j in range(PASS_BANKS):
+                empty_bank(g, j, transpose_bank(g, j))
+            if g >= 1:
+                quantise_pass(g - 1)
+            c, i = home[g]
+            passes = widths[c] // K_PASS
+            if c + 1 < len(widths):
                 for operand in range(2):
-                    order_words(c, operand)
-                if c + PREFETCH < len(widths):
-                    load_chunk(c + PREFETCH)
+                    if operand * passes // 2 == i:
+                        order_chunk(c + 1, operand)
 
-        order_round(0)
-        for r in range(ROUNDS):
-            for g in range(r * ROUND_PASSES, (r + 1) * ROUND_PASSES):
-                grouped[g] = group_pool.tile(
-                    [P, (ROWS + FEATURES) * PACK], BF16, align_bytes=64, tag="grouped", name="grouped"
-                )
-                for j in range(PASS_BANKS):
-                    empty_bank(g, j, transpose_bank(g, j))
-                if r >= 1:
-                    quantise_pass(g - ROUND_PASSES)
-            if r + 1 < ROUNDS:
-                order_round(r + 1)
-
-            if r == LAG - 1:
+            if g == 0:
                 nc.scalar.copy(
                     out=scale_bc[:].rearrange("m (p j) -> m p j", j=PER_PARTITION),
                     in_=spread_over_partitions(scale_col, "acc0"),
@@ -217,16 +214,14 @@ def tile_modelnew_k_kernel(
                 )
                 for b in range(BLOCKS):
                     acc.append(acc_psum.tile([P, FEATURES], F32, tag="acc%d" % b, name="acc%d" % b))
-            if r in prepare_in_round:
-                prepare_row_block(prepare_in_round[r])
+            if g in prepare_after_pass:
+                prepare_row_block(prepare_after_pass[g])
 
-            if r >= LAG:
-                for g in range((r - LAG) * ROUND_PASSES, (r - LAG + 1) * ROUND_PASSES):
-                    multiply_pass(g)
+            if g >= LAG:
+                multiply_pass(g - LAG)
 
-        for g in range(PASSES - ROUND_PASSES, PASSES):
-            quantise_pass(g)
-        for g in range(PASSES - LAG * ROUND_PASSES, PASSES):
+        quantise_pass(PASSES - 1)
+        for g in range(PASSES - LAG, PASSES):
             multiply_pass(g)
 
         for b in range(BLOCKS):

@@ -14,6 +14,7 @@ P = 128
 PACK = 4
 K_PASS = P * PACK
 BANK = 512
+HALF = 16
 
 ROWS = 512
 FEATURES = 512
@@ -21,14 +22,13 @@ K = 16384
 EPS = 1e-5
 BLOCKS = ROWS // P
 PASSES = K // K_PASS
-WORDS = K_PASS // 2
 PER_PARTITION = FEATURES // P
 
 CHUNK_MAX = 1024
 PREFETCH = 5
 LAG = 2
-PASS_BANKS = 4
-HALF = 16
+LAST = 4
+TURN_BANKS = 4
 
 FLOPS = 2 * ROWS * FEATURES * K
 
@@ -47,8 +47,7 @@ def tile_modelnew_k_kernel(
     nc = tc.nc
     widths = chunk_widths()
     home = [(c, i) for c, width in enumerate(widths) for i in range(width // K_PASS)]
-    x_view = x.rearrange("(b p) k -> p b k", p=P)
-    w_view = weight.rearrange("(b p) k -> p b k", p=P)
+    views = [m.rearrange("(b p) k -> p b k", p=P) for m in (x, weight)]
     y_view = y.rearrange("(b p) n -> p b n", p=P)
 
     with ExitStack() as ctx:
@@ -57,29 +56,24 @@ def tile_modelnew_k_kernel(
         order_pool = ctx.enter_context(tc.tile_pool(name="ordered", bufs=3))
         group_pool = ctx.enter_context(tc.tile_pool(name="grouped", bufs=3))
         code_pool = ctx.enter_context(tc.tile_pool(name="codes", bufs=LAG + 2))
+        last_pool = ctx.enter_context(tc.tile_pool(name="last", bufs=LAST))
         result_pool = ctx.enter_context(tc.tile_pool(name="result", bufs=BLOCKS))
-        turn_psum = ctx.enter_context(tc.psum_pool(name="turn", bufs=PASS_BANKS))
+        turn_psum = ctx.enter_context(tc.psum_pool(name="turn", bufs=TURN_BANKS))
         acc_psum = ctx.enter_context(tc.psum_pool(name="acc", bufs=1))
         ctx.enter_context(tc.manual_schedule())
 
         staged = {}
         ordered = {}
-        grouped = {}
-        quantised = {}
 
         def load_chunk(c):
             k0, width = sum(widths[:c]), widths[c]
-            x_st = stage.tile([P, BLOCKS * width], BF16, tag="x_st")
-            nc.sync.dma_start(
-                out=x_st[:].rearrange("p (b k) -> p b k", b=BLOCKS),
-                in_=x_view[:, :, k0 : k0 + width],
-            )
-            w_st = stage.tile([P, BLOCKS * width], BF16, tag="w_st")
-            nc.sync.dma_start(
-                out=w_st[:].rearrange("p (b k) -> p b k", b=BLOCKS),
-                in_=w_view[:, :, k0 : k0 + width],
-            )
-            staged[c] = (x_st, w_st)
+            for operand in range(2):
+                tile = stage.tile([P, BLOCKS * width], BF16, tag="staged%d" % operand, name="staged")
+                nc.sync.dma_start(
+                    out=tile[:].rearrange("p (b k) -> p b k", b=BLOCKS),
+                    in_=views[operand][:, :, k0 : k0 + width],
+                )
+                staged[c, operand] = tile
 
         def load_vector(vector, name):
             column = consts.tile([P, PER_PARTITION], BF16, name=name)
@@ -103,130 +97,167 @@ def tile_modelnew_k_kernel(
         scale_col = consts.tile([P, PER_PARTITION], F32)
         shift_col = consts.tile([P, PER_PARTITION], F32)
         nc.scalar.activation(out=scale_col[:], in_=var_col[:], func=SQRT, bias=EPS)
-        nc.vector.reciprocal(out=scale_col[:], in_=scale_col[:])
-        nc.vector.tensor_mul(out=scale_col[:], in0=scale_col[:], in1=gain_col[:])
-        nc.vector.tensor_sub(out=shift_col[:], in0=bias_col[:], in1=mean_col[:])
-        nc.vector.tensor_mul(out=shift_col[:], in0=shift_col[:], in1=scale_col[:])
-        nc.vector.tensor_add(out=shift_col[:], in0=shift_col[:], in1=offset_col[:])
+
+        def finish_columns():
+            nc.vector.reciprocal(out=scale_col[:], in_=scale_col[:])
+            nc.vector.tensor_mul(out=scale_col[:], in0=scale_col[:], in1=gain_col[:])
+            nc.vector.tensor_sub(out=shift_col[:], in0=bias_col[:], in1=mean_col[:])
+            nc.vector.tensor_mul(out=shift_col[:], in0=shift_col[:], in1=scale_col[:])
+            nc.vector.tensor_add(out=shift_col[:], in0=shift_col[:], in1=offset_col[:])
 
         scale_bc = consts.tile([P, FEATURES], F32)
         shift_bc = consts.tile([P, FEATURES], F32)
 
-        def spread_over_partitions(column, tag):
+        def spread_over_partitions(column, row, tag):
             bank = acc_psum.tile([P, BANK], F32, tag=tag, name="spread")
             for j in range(PER_PARTITION):
                 nc.tensor.transpose(
                     bank[:, j * P : (j + 1) * P], column[:, j : j + 1].to_broadcast([P, P]), ident[:]
                 )
-            return bank[:].rearrange("m (j p) -> m p j", j=PER_PARTITION)
+            nc.scalar.copy(
+                out=row[:].rearrange("m (p j) -> m p j", j=PER_PARTITION),
+                in_=bank[:].rearrange("m (j p) -> m p j", j=PER_PARTITION),
+            )
 
         factor = consts.tile([P, BLOCKS * FEATURES], F32)
         addend = consts.tile([P, BLOCKS * FEATURES], F32)
 
-        def prepare_row_block(b):
+        def prepare(b, step):
             cols = slice(b * FEATURES, (b + 1) * FEATURES)
-            nc.vector.tensor_mul(out=factor[:, cols], in0=scale_bc[:], in1=y_sb[:, cols])
-            nc.vector.tensor_add(out=addend[:, cols], in0=shift_bc[:], in1=y_sb[:, cols])
-            nc.vector.tensor_mul(out=addend[:, cols], in0=addend[:, cols], in1=y_sb[:, cols])
+            if step == 0:
+                nc.vector.tensor_add(out=addend[:, cols], in0=shift_bc[:], in1=y_sb[:, cols])
+            elif step == 1:
+                nc.vector.tensor_mul(out=factor[:, cols], in0=scale_bc[:], in1=y_sb[:, cols])
+            else:
+                nc.vector.tensor_mul(out=addend[:, cols], in0=addend[:, cols], in1=y_sb[:, cols])
 
-        first_free = sum(widths[:PREFETCH]) // K_PASS
-        prepare_after_pass = {first_free + 4 * b: b for b in range(BLOCKS)}
+        steps = [(b, step) for b in range(BLOCKS) for step in range(3)]
+        prepare_in_pass = {sum(widths[:PREFETCH]) // K_PASS + n: bs for n, bs in enumerate(steps)}
 
-        def order_words(c, operand):
+        def order_chunk(c, operand):
             tile = order_pool.tile([P, BLOCKS * widths[c]], BF16, tag="ordered%d" % operand, name="ordered")
-            source = staged[c][operand][:].rearrange("p (m q u e) -> p u m q e", q=P // 8, u=2, e=HALF)
+            source = staged[c, operand][:].rearrange("p (m q u e) -> p u m q e", q=P // 8, u=2, e=HALF)
             target = tile[:].rearrange("p (u m q e) -> p u m q e", u=2, q=P // 8, e=HALF)
             for u in range(2):
                 nc.vector.tensor_copy(out=target[:, u], in_=source[:, u])
-            ordered.setdefault(c, []).append(tile)
+            ordered[c, operand] = tile
+            if operand == 1 and c + PREFETCH < len(widths):
+                load_chunk(c + PREFETCH)
 
-        def transpose_bank(g, j):
-            c, i = home[g]
-            words = ordered[c][j // 2][:].bitcast(F32)
-            passes = widths[c] // K_PASS
-            bank = turn_psum.tile([P, BANK], F32, tag="bank")
-            for h in range(2):
+        def turn(first, second, grouped, place):
+            bank = turn_psum.tile([P, BANK], F32, tag="bank", name="bank")
+            for h, (g, operand, b) in enumerate((first, second)):
+                c, i = home[g]
+                words = ordered[c, operand][:].bitcast(F32)
                 for u in range(2):
-                    w0 = ((u * BLOCKS + 2 * (j % 2) + h) * passes + i) * P
+                    w0 = ((u * BLOCKS + b) * (widths[c] // K_PASS) + i) * P
                     q = 2 * h + u
                     nc.tensor.transpose(bank[:, q * P : (q + 1) * P], words[:, w0 : w0 + P], ident[:])
-            return bank
-
-        def empty_bank(g, j, bank):
             nc.scalar.copy(
-                out=grouped[g][:]
-                .bitcast(F32)[:, j * BANK : (j + 1) * BANK]
+                out=grouped[:]
+                .bitcast(F32)[:, place * BANK : (place + 1) * BANK]
                 .rearrange("p (h r u) -> p h r u", h=2, u=2),
                 in_=bank[:].rearrange("p (h u r) -> p h r u", h=2, u=2),
             )
 
-        def quantise_pass(g):
-            words = code_pool.tile([P, ROWS + FEATURES], U32, align_bytes=64, tag="words")
-            scales = code_pool.tile([P, ROWS + FEATURES], U8, align_bytes=64, tag="scales")
-            nc.vector.quantize_mx(out=words[:].bitcast(FP8X4), scales=scales[:], in_=grouped[g][:])
-            quantised[g] = (words, scales)
+        def group_tile(columns):
+            return group_pool.tile([P, columns * PACK], BF16, align_bytes=64, tag="grouped", name="grouped")
+
+        def quantise(pool, grouped, columns):
+            words = pool.tile([P, columns], U32, align_bytes=64, tag="words", name="words")
+            scales = pool.tile([P, columns], U8, align_bytes=64, tag="scales", name="scales")
+            nc.vector.quantize_mx(out=words[:].bitcast(FP8X4), scales=scales[:], in_=grouped[:])
+            return words, scales
 
         acc = []
 
-        def multiply_pass(g):
-            words, scales = quantised[g]
-            for b in range(BLOCKS):
-                nc.tensor.matmul_mx(
-                    out=acc[b][:],
-                    lhsT=words[:, b * P : (b + 1) * P].bitcast(FP8X4),
-                    lhsT_scale=scales[:, b * P : (b + 1) * P],
-                    rhs=words[:, ROWS : ROWS + FEATURES].bitcast(FP8X4),
-                    rhs_scale=scales[:, ROWS : ROWS + FEATURES],
-                    start=(g == 0),
-                    stop=(g == PASSES - 1),
-                )
+        def multiply(g, b, left, l0, right, r0):
+            nc.tensor.matmul_mx(
+                out=acc[b][:],
+                lhsT=left[0][:, l0 : l0 + P].bitcast(FP8X4),
+                lhsT_scale=left[1][:, l0 : l0 + P],
+                rhs=right[0][:, r0 : r0 + FEATURES].bitcast(FP8X4),
+                rhs_scale=right[1][:, r0 : r0 + FEATURES],
+                start=(g == 0),
+                stop=(g == PASSES - 1),
+            )
 
-        def order_chunk(c, operand):
-            order_words(c, operand)
-            if operand == 1 and c + PREFETCH < len(widths):
-                load_chunk(c + PREFETCH)
+        grouped = {}
+        quantised = {}
+
+        def multiply_pass(g):
+            for b in range(BLOCKS):
+                multiply(g, b, quantised[g], b * P, quantised[g], ROWS)
 
         order_chunk(0, 0)
         order_chunk(0, 1)
-        for g in range(PASSES):
-            grouped[g] = group_pool.tile(
-                [P, (ROWS + FEATURES) * PACK], BF16, align_bytes=64, tag="grouped", name="grouped"
-            )
-            for j in range(PASS_BANKS):
-                empty_bank(g, j, transpose_bank(g, j))
-            if g >= 1:
-                quantise_pass(g - 1)
+        first_last = PASSES - LAST
+        for g in range(first_last):
+            grouped[g] = group_tile(ROWS + FEATURES)
+            for j in range(TURN_BANKS):
+                b = 2 * (j % 2)
+                turn((g, j // 2, b), (g, j // 2, b + 1), grouped[g], j)
             c, i = home[g]
-            passes = widths[c] // K_PASS
-            if c + 1 < len(widths):
-                for operand in range(2):
-                    if operand * passes // 2 == i:
-                        order_chunk(c + 1, operand)
-
+            for operand in range(2):
+                if operand * (widths[c] // K_PASS) // 2 == i:
+                    order_chunk(c + 1, operand)
+            if g >= 1:
+                quantised[g - 1] = quantise(code_pool, grouped[g - 1], ROWS + FEATURES)
+            if g in prepare_in_pass:
+                prepare(*prepare_in_pass[g])
             if g == 0:
-                nc.scalar.copy(
-                    out=scale_bc[:].rearrange("m (p j) -> m p j", j=PER_PARTITION),
-                    in_=spread_over_partitions(scale_col, "acc0"),
-                )
-                nc.vector.tensor_copy(
-                    out=shift_bc[:].rearrange("m (p j) -> m p j", j=PER_PARTITION),
-                    in_=spread_over_partitions(shift_col, "acc1"),
-                )
+                finish_columns()
+            if g == LAG - 1:
+                spread_over_partitions(scale_col, scale_bc, "acc0")
+                spread_over_partitions(shift_col, shift_bc, "acc1")
                 for b in range(BLOCKS):
                     acc.append(acc_psum.tile([P, FEATURES], F32, tag="acc%d" % b, name="acc%d" % b))
-            if g in prepare_after_pass:
-                prepare_row_block(prepare_after_pass[g])
-
             if g >= LAG:
                 multiply_pass(g - LAG)
 
-        quantise_pass(PASSES - 1)
-        for g in range(PASSES - LAG, PASSES):
-            multiply_pass(g)
+        last_passes = range(first_last, PASSES)
+        weight_codes = {}
+        x_codes = {}
 
-        for b in range(BLOCKS):
+        def last_weight(g):
+            tile = group_tile(FEATURES)
+            for place in range(2):
+                turn((g, 1, 2 * place), (g, 1, 2 * place + 1), tile, place)
+            return tile
+
+        def last_x(b):
+            tile = group_tile(LAST * P)
+            for place in range(LAST // 2):
+                g = first_last + 2 * place
+                turn((g, 0, b), (g + 1, 0, b), tile, place)
+            return tile
+
+        def finish_row_block(b):
+            for n, g in enumerate(last_passes):
+                multiply(g, b, x_codes[b], n * P, weight_codes[g], 0)
             cols = slice(b * FEATURES, (b + 1) * FEATURES)
-            result = result_pool.tile([P, FEATURES], F32)
+            result = result_pool.tile([P, FEATURES], F32, tag="result", name="result")
             nc.vector.tensor_mul(out=result[:], in0=acc[b][:], in1=factor[:, cols])
             nc.vector.tensor_add(out=result[:], in0=result[:], in1=addend[:, cols])
             nc.sync.dma_start(out=out[b * P : (b + 1) * P, :], in_=result[:])
+
+        tiles = {}
+        for g in last_passes:
+            tiles[g] = last_weight(g)
+            if g == first_last:
+                c = home[g][0]
+                order_chunk(c + 1, 1)
+                quantised[g - 1] = quantise(code_pool, grouped[g - 1], ROWS + FEATURES)
+            else:
+                weight_codes[g - 1] = quantise(last_pool, tiles[g - 1], FEATURES)
+            if g == first_last + 1:
+                multiply_pass(first_last - LAG)
+                order_chunk(c + 1, 0)
+        x_tile = last_x(0)
+        weight_codes[PASSES - 1] = quantise(last_pool, tiles[PASSES - 1], FEATURES)
+        multiply_pass(first_last - 1)
+        for b in range(BLOCKS):
+            x_codes[b] = quantise(code_pool, x_tile, LAST * P)
+            if b + 1 < BLOCKS:
+                x_tile = last_x(b + 1)
+            finish_row_block(b)

@@ -15,6 +15,7 @@ PACK = 4
 K_PASS = P * PACK
 BANK = 512
 HALF = 16
+RUN = 256
 
 ROWS = 512
 FEATURES = 512
@@ -25,7 +26,8 @@ PASSES = K // K_PASS
 PER_PARTITION = FEATURES // P
 
 CHUNK_MAX = 1024
-PREFETCH = 5
+NARROW_CHUNKS = 4
+PREFETCH = 6
 LAG = 2
 LAST = 4
 TURN_BANKS = 4
@@ -34,9 +36,8 @@ FLOPS = 2 * ROWS * FEATURES * K
 
 
 def chunk_widths():
-    widths = [K_PASS]
-    while sum(widths) < K:
-        widths.append(min(sum(widths), CHUNK_MAX))
+    widths = [K_PASS] * NARROW_CHUNKS
+    widths += [CHUNK_MAX] * ((K - sum(widths)) // CHUNK_MAX)
     assert sum(widths) == K
     return widths
 
@@ -63,7 +64,7 @@ def tile_modelnew_k_kernel(
         ctx.enter_context(tc.manual_schedule())
 
         staged = {}
-        ordered = {}
+        odd_run = {}
 
         def load_chunk(c):
             k0, width = sum(widths[:c]), widths[c]
@@ -134,23 +135,30 @@ def tile_modelnew_k_kernel(
         steps = [(b, step) for b in range(BLOCKS) for step in range(3)]
         prepare_in_pass = {sum(widths[:PREFETCH]) // K_PASS + n: bs for n, bs in enumerate(steps)}
 
-        def order_chunk(c, operand):
-            tile = order_pool.tile([P, BLOCKS * widths[c]], BF16, tag="ordered%d" % operand, name="ordered")
-            source = staged[c, operand][:].rearrange("p (m q u e) -> p u m q e", q=P // 8, u=2, e=HALF)
-            target = tile[:].rearrange("p (u m q e) -> p u m q e", u=2, q=P // 8, e=HALF)
-            for u in range(2):
-                nc.vector.tensor_copy(out=target[:, u], in_=source[:, u])
-            ordered[c, operand] = tile
-            if operand == 1 and c + PREFETCH < len(widths):
-                load_chunk(c + PREFETCH)
+        def half_blocks(c, operand):
+            return staged[c, operand][:].rearrange(
+                "p (m run s par e) -> p m run s par e", run=2, s=RUN // HALF // 2, par=2, e=HALF
+            )
+
+        def make_odd_run(c, operand):
+            tile = order_pool.tile([P, BLOCKS * widths[c] // 2], BF16, tag="odd%d" % operand, name="odd_run")
+            nc.vector.tensor_copy(
+                out=tile[:].rearrange("p (m s run e) -> p m s run e", s=RUN // HALF // 2, run=2, e=HALF),
+                in_=half_blocks(c, operand)[:, :, :, :, 1].rearrange("p m run s e -> p m s run e"),
+            )
+            odd_run[c, operand] = tile
+
+        def mend_even_run(c, operand):
+            halves = half_blocks(c, operand)
+            nc.vector.tensor_copy(out=halves[:, :, 0, :, 1], in_=halves[:, :, 1, :, 0])
 
         def turn(first, second, grouped, place):
             bank = turn_psum.tile([P, BANK], F32, tag="bank", name="bank")
             for h, (g, operand, b) in enumerate((first, second)):
                 c, i = home[g]
-                words = ordered[c, operand][:].bitcast(F32)
-                for u in range(2):
-                    w0 = ((u * BLOCKS + b) * (widths[c] // K_PASS) + i) * P
+                m = b * (widths[c] // K_PASS) + i
+                for u, (tile, w0) in enumerate(((staged[c, operand], 2 * m * P), (odd_run[c, operand], m * P))):
+                    words = tile[:].bitcast(F32)
                     q = 2 * h + u
                     nc.tensor.transpose(bank[:, q * P : (q + 1) * P], words[:, w0 : w0 + P], ident[:])
             nc.scalar.copy(
@@ -189,8 +197,9 @@ def tile_modelnew_k_kernel(
             for b in range(BLOCKS):
                 multiply(g, b, quantised[g], b * P, quantised[g], ROWS)
 
-        order_chunk(0, 0)
-        order_chunk(0, 1)
+        for operand in range(2):
+            make_odd_run(0, operand)
+            mend_even_run(0, operand)
         first_last = PASSES - LAST
         for g in range(first_last):
             grouped[g] = group_tile(ROWS + FEATURES)
@@ -198,11 +207,15 @@ def tile_modelnew_k_kernel(
                 b = 2 * (j % 2)
                 turn((g, j // 2, b), (g, j // 2, b + 1), grouped[g], j)
             c, i = home[g]
-            for operand in range(2):
-                if operand * (widths[c] // K_PASS) // 2 == i:
-                    order_chunk(c + 1, operand)
+            passes = widths[c] // K_PASS
+            next_operands = [operand for operand in range(2) if operand * passes // 2 == i]
+            for operand in next_operands:
+                make_odd_run(c + 1, operand)
+                mend_even_run(c + 1, operand)
             if g >= 1:
                 quantised[g - 1] = quantise(code_pool, grouped[g - 1], ROWS + FEATURES)
+            if i == passes - 1 and c + PREFETCH < len(widths):
+                load_chunk(c + PREFETCH)
             if g in prepare_in_pass:
                 prepare(*prepare_in_pass[g])
             if g == 0:
@@ -232,9 +245,11 @@ def tile_modelnew_k_kernel(
                 turn((g, 0, b), (g + 1, 0, b), tile, place)
             return tile
 
-        def finish_row_block(b):
+        def multiply_row_block(b):
             for n, g in enumerate(last_passes):
                 multiply(g, b, x_codes[b], n * P, weight_codes[g], 0)
+
+        def finish_row_block(b):
             cols = slice(b * FEATURES, (b + 1) * FEATURES)
             result = result_pool.tile([P, FEATURES], F32, tag="result", name="result")
             nc.vector.tensor_mul(out=result[:], in0=acc[b][:], in1=factor[:, cols])
@@ -246,13 +261,15 @@ def tile_modelnew_k_kernel(
             tiles[g] = last_weight(g)
             if g == first_last:
                 c = home[g][0]
-                order_chunk(c + 1, 1)
+                make_odd_run(c + 1, 1)
                 quantised[g - 1] = quantise(code_pool, grouped[g - 1], ROWS + FEATURES)
+                mend_even_run(c + 1, 1)
+                make_odd_run(c + 1, 0)
             else:
                 weight_codes[g - 1] = quantise(last_pool, tiles[g - 1], FEATURES)
             if g == first_last + 1:
                 multiply_pass(first_last - LAG)
-                order_chunk(c + 1, 0)
+                mend_even_run(c + 1, 0)
         x_tile = last_x(0)
         weight_codes[PASSES - 1] = quantise(last_pool, tiles[PASSES - 1], FEATURES)
         multiply_pass(first_last - 1)
@@ -260,4 +277,7 @@ def tile_modelnew_k_kernel(
             x_codes[b] = quantise(code_pool, x_tile, LAST * P)
             if b + 1 < BLOCKS:
                 x_tile = last_x(b + 1)
-            finish_row_block(b)
+            if b >= 1:
+                finish_row_block(b - 1)
+            multiply_row_block(b)
+        finish_row_block(BLOCKS - 1)

@@ -8,7 +8,6 @@ BF16 = mybir.dt.bfloat16
 U32 = mybir.dt.uint32
 U8 = mybir.dt.uint8
 FP8X4 = mybir.dt.float8_e4m3fn_x4
-SQRT = mybir.ActivationFunctionType.Sqrt
 
 P = 128
 PACK = 4
@@ -28,6 +27,7 @@ PER_PARTITION = FEATURES // P
 CHUNK_MAX = 1024
 NARROW_CHUNKS = 4
 PREFETCH = 6
+COLUMNS_FROM = 8
 LAG = 2
 LAST = 4
 TURN_BANKS = 4
@@ -66,21 +66,27 @@ def tile_modelnew_k_kernel(
         staged = {}
         odd_run = {}
 
+        def pieces(c):
+            return [slice(0, 2), slice(2, 4)] if c == 0 else [slice(0, BLOCKS)]
+
         def load_chunk(c):
             k0, width = sum(widths[:c]), widths[c]
             for operand in range(2):
                 tile = stage.tile([P, BLOCKS * width], BF16, tag="staged%d" % operand, name="staged")
-                nc.sync.dma_start(
-                    out=tile[:].rearrange("p (b k) -> p b k", b=BLOCKS),
-                    in_=views[operand][:, :, k0 : k0 + width],
-                )
+                for blocks in pieces(c):
+                    nc.sync.dma_start(
+                        out=tile[:].rearrange("p (b k) -> p b k", b=BLOCKS)[:, blocks],
+                        in_=views[operand][:, blocks, k0 : k0 + width],
+                    )
                 staged[c, operand] = tile
 
         def load_vector(vector, name):
             column = consts.tile([P, PER_PARTITION], BF16, name=name)
-            nc.scalar.dma_start(out=column[:], in_=vector.rearrange("(p j) -> p j", j=PER_PARTITION))
+            nc.gpsimd.dma_start(out=column[:], in_=vector.rearrange("(p j) -> p j", j=PER_PARTITION))
             return column
 
+        ident = consts.tile([P, P], F32)
+        make_identity(nc, ident[:])
         var_col = load_vector(running_var, "var_col")
         gain_col = load_vector(norm_weight, "gain_col")
         bias_col = load_vector(bias, "bias_col")
@@ -92,15 +98,18 @@ def tile_modelnew_k_kernel(
         y_sb = consts.tile([P, BLOCKS * FEATURES], BF16)
         nc.sync.dma_start(out=y_sb[:].rearrange("p (b n) -> p b n", b=BLOCKS), in_=y_view)
 
-        ident = consts.tile([P, P], F32)
-        make_identity(nc, ident[:])
-
         scale_col = consts.tile([P, PER_PARTITION], F32)
         shift_col = consts.tile([P, PER_PARTITION], F32)
-        nc.scalar.activation(out=scale_col[:], in_=var_col[:], func=SQRT, bias=EPS)
+        exponent = consts.tile([P, PER_PARTITION], F32)
+        nc.gpsimd.memset(exponent[:], -0.5)
+        nc.gpsimd.tensor_scalar(
+            out=scale_col[:], in0=var_col[:], scalar1=EPS, scalar2=None, op0=mybir.AluOpType.add
+        )
+        nc.gpsimd.tensor_tensor(
+            out=scale_col[:], in0=scale_col[:], in1=exponent[:], op=mybir.AluOpType.pow
+        )
 
         def finish_columns():
-            nc.vector.reciprocal(out=scale_col[:], in_=scale_col[:])
             nc.vector.tensor_mul(out=scale_col[:], in0=scale_col[:], in1=gain_col[:])
             nc.vector.tensor_sub(out=shift_col[:], in0=bias_col[:], in1=mean_col[:])
             nc.vector.tensor_mul(out=shift_col[:], in0=shift_col[:], in1=scale_col[:])
@@ -109,8 +118,8 @@ def tile_modelnew_k_kernel(
         scale_bc = consts.tile([P, FEATURES], F32)
         shift_bc = consts.tile([P, FEATURES], F32)
 
-        def spread_over_partitions(column, row, tag):
-            bank = acc_psum.tile([P, BANK], F32, tag=tag, name="spread")
+        def spread_over_partitions(column, row):
+            bank = turn_psum.tile([P, BANK], F32, tag="bank", name="bank")
             for j in range(PER_PARTITION):
                 nc.tensor.transpose(
                     bank[:, j * P : (j + 1) * P], column[:, j : j + 1].to_broadcast([P, P]), ident[:]
@@ -133,26 +142,28 @@ def tile_modelnew_k_kernel(
                 nc.vector.tensor_mul(out=addend[:, cols], in0=addend[:, cols], in1=y_sb[:, cols])
 
         steps = [(b, step) for b in range(BLOCKS) for step in range(3)]
-        prepare_in_pass = {sum(widths[:PREFETCH]) // K_PASS + n: bs for n, bs in enumerate(steps)}
+        prepare_in_pass = {COLUMNS_FROM + 2 + n: bs for n, bs in enumerate(steps)}
+        assert COLUMNS_FROM >= sum(widths[:PREFETCH]) // K_PASS
 
         def half_blocks(c, operand):
             return staged[c, operand][:].rearrange(
                 "p (m run s par e) -> p m run s par e", run=2, s=RUN // HALF // 2, par=2, e=HALF
             )
 
-        def make_odd_run(c, operand):
+        def put_in_order(c, operand):
             tile = order_pool.tile([P, BLOCKS * widths[c] // 2], BF16, tag="odd%d" % operand, name="odd_run")
-            nc.vector.tensor_copy(
-                out=tile[:].rearrange("p (m s run e) -> p m s run e", s=RUN // HALF // 2, run=2, e=HALF),
-                in_=half_blocks(c, operand)[:, :, :, :, 1].rearrange("p m run s e -> p m s run e"),
-            )
+            odd = tile[:].rearrange("p (m s run e) -> p m s run e", s=RUN // HALF // 2, run=2, e=HALF)
+            halves = half_blocks(c, operand)
+            for blocks in pieces(c):
+                passes = widths[c] // K_PASS
+                m = slice(blocks.start * passes, blocks.stop * passes)
+                nc.vector.tensor_copy(
+                    out=odd[:, m], in_=halves[:, m, :, :, 1].rearrange("p m run s e -> p m s run e")
+                )
+                nc.vector.tensor_copy(out=halves[:, m, 0, :, 1], in_=halves[:, m, 1, :, 0])
             odd_run[c, operand] = tile
 
-        def mend_even_run(c, operand):
-            halves = half_blocks(c, operand)
-            nc.vector.tensor_copy(out=halves[:, :, 0, :, 1], in_=halves[:, :, 1, :, 0])
-
-        def turn(first, second, grouped, place):
+        def turn(first, second, grouped, place, copy=nc.scalar.copy):
             bank = turn_psum.tile([P, BANK], F32, tag="bank", name="bank")
             for h, (g, operand, b) in enumerate((first, second)):
                 c, i = home[g]
@@ -161,7 +172,7 @@ def tile_modelnew_k_kernel(
                     words = tile[:].bitcast(F32)
                     q = 2 * h + u
                     nc.tensor.transpose(bank[:, q * P : (q + 1) * P], words[:, w0 : w0 + P], ident[:])
-            nc.scalar.copy(
+            copy(
                 out=grouped[:]
                 .bitcast(F32)[:, place * BANK : (place + 1) * BANK]
                 .rearrange("p (h r u) -> p h r u", h=2, u=2),
@@ -178,6 +189,8 @@ def tile_modelnew_k_kernel(
             return words, scales
 
         acc = []
+        for b in range(BLOCKS):
+            acc.append(acc_psum.tile([P, FEATURES], F32, tag="acc%d" % b, name="acc%d" % b))
 
         def multiply(g, b, left, l0, right, r0):
             nc.tensor.matmul_mx(
@@ -198,8 +211,7 @@ def tile_modelnew_k_kernel(
                 multiply(g, b, quantised[g], b * P, quantised[g], ROWS)
 
         for operand in range(2):
-            make_odd_run(0, operand)
-            mend_even_run(0, operand)
+            put_in_order(0, operand)
         first_last = PASSES - LAST
         for g in range(first_last):
             grouped[g] = group_tile(ROWS + FEATURES)
@@ -210,21 +222,18 @@ def tile_modelnew_k_kernel(
             passes = widths[c] // K_PASS
             next_operands = [operand for operand in range(2) if operand * passes // 2 == i]
             for operand in next_operands:
-                make_odd_run(c + 1, operand)
-                mend_even_run(c + 1, operand)
+                put_in_order(c + 1, operand)
             if g >= 1:
                 quantised[g - 1] = quantise(code_pool, grouped[g - 1], ROWS + FEATURES)
             if i == passes - 1 and c + PREFETCH < len(widths):
                 load_chunk(c + PREFETCH)
             if g in prepare_in_pass:
                 prepare(*prepare_in_pass[g])
-            if g == 0:
+            if g == COLUMNS_FROM:
                 finish_columns()
-            if g == LAG - 1:
-                spread_over_partitions(scale_col, scale_bc, "acc0")
-                spread_over_partitions(shift_col, shift_bc, "acc1")
-                for b in range(BLOCKS):
-                    acc.append(acc_psum.tile([P, FEATURES], F32, tag="acc%d" % b, name="acc%d" % b))
+            if g == COLUMNS_FROM + 1:
+                spread_over_partitions(scale_col, scale_bc)
+                spread_over_partitions(shift_col, shift_bc)
             if g >= LAG:
                 multiply_pass(g - LAG)
 
@@ -235,7 +244,8 @@ def tile_modelnew_k_kernel(
         def last_weight(g):
             tile = group_tile(FEATURES)
             for place in range(2):
-                turn((g, 1, 2 * place), (g, 1, 2 * place + 1), tile, place)
+                copy = nc.vector.tensor_copy if place == 1 and g == PASSES - 1 else nc.scalar.copy
+                turn((g, 1, 2 * place), (g, 1, 2 * place + 1), tile, place, copy)
             return tile
 
         def last_x(b):
@@ -250,34 +260,40 @@ def tile_modelnew_k_kernel(
                 multiply(g, b, x_codes[b], n * P, weight_codes[g], 0)
 
         def finish_row_block(b):
-            cols = slice(b * FEATURES, (b + 1) * FEATURES)
             result = result_pool.tile([P, FEATURES], F32, tag="result", name="result")
-            nc.vector.tensor_mul(out=result[:], in0=acc[b][:], in1=factor[:, cols])
-            nc.vector.tensor_add(out=result[:], in0=result[:], in1=addend[:, cols])
-            nc.sync.dma_start(out=out[b * P : (b + 1) * P, :], in_=result[:])
+            width = FEATURES // 2
+            for n in range(0, FEATURES, width):
+                f0 = b * FEATURES + n
+                nc.vector.tensor_mul(
+                    out=result[:, n : n + width], in0=acc[b][:, n : n + width], in1=factor[:, f0 : f0 + width]
+                )
+            for n in range(0, FEATURES, width):
+                f0 = b * FEATURES + n
+                nc.vector.tensor_add(
+                    out=result[:, n : n + width], in0=result[:, n : n + width], in1=addend[:, f0 : f0 + width]
+                )
+                nc.sync.dma_start(out=out[b * P : (b + 1) * P, n : n + width], in_=result[:, n : n + width])
 
         tiles = {}
         for g in last_passes:
             tiles[g] = last_weight(g)
             if g == first_last:
                 c = home[g][0]
-                make_odd_run(c + 1, 1)
+                put_in_order(c + 1, 1)
                 quantised[g - 1] = quantise(code_pool, grouped[g - 1], ROWS + FEATURES)
-                mend_even_run(c + 1, 1)
-                make_odd_run(c + 1, 0)
             else:
                 weight_codes[g - 1] = quantise(last_pool, tiles[g - 1], FEATURES)
             if g == first_last + 1:
                 multiply_pass(first_last - LAG)
-                mend_even_run(c + 1, 0)
+                put_in_order(c + 1, 0)
         x_tile = last_x(0)
         weight_codes[PASSES - 1] = quantise(last_pool, tiles[PASSES - 1], FEATURES)
         multiply_pass(first_last - 1)
         for b in range(BLOCKS):
             x_codes[b] = quantise(code_pool, x_tile, LAST * P)
-            if b + 1 < BLOCKS:
-                x_tile = last_x(b + 1)
             if b >= 1:
                 finish_row_block(b - 1)
+            if b + 1 < BLOCKS:
+                x_tile = last_x(b + 1)
             multiply_row_block(b)
         finish_row_block(BLOCKS - 1)

@@ -24,40 +24,35 @@ BLOCKS = ROWS // P
 PASSES = K // K_PASS
 PER_PARTITION = FEATURES // P
 
-CHUNK_MAX = 1024
-NARROW_CHUNKS = 4
-PREFETCH = 6
-COLUMNS_FROM = 8
-LAG = 2
-LAST = 4
+CHUNK_PASSES = 4
+CHUNK = CHUNK_PASSES * K_PASS
+PIECE_BLOCKS = 2
+SETS = PIECE_BLOCKS * CHUNK_PASSES
+PIECES = 4
+ROUNDS = PASSES // CHUNK_PASSES * PIECES
+WIDE = SETS * P
+LAG = PIECES + 1
+PREFETCH = 12
+VECTORS_BEHIND = 8
+COLUMNS_FROM = VECTORS_BEHIND + 2
 TURN_BANKS = 4
 
 FLOPS = 2 * ROWS * FEATURES * K
-
-
-def chunk_widths():
-    widths = [K_PASS] * NARROW_CHUNKS
-    widths += [CHUNK_MAX] * ((K - sum(widths)) // CHUNK_MAX)
-    assert sum(widths) == K
-    return widths
 
 
 def tile_modelnew_k_kernel(
     tc, x, y, weight, bias, running_mean, running_var, norm_weight, norm_bias, out
 ):
     nc = tc.nc
-    widths = chunk_widths()
-    home = [(c, i) for c, width in enumerate(widths) for i in range(width // K_PASS)]
-    views = [m.rearrange("(b p) k -> p b k", p=P) for m in (x, weight)]
-    y_view = y.rearrange("(b p) n -> p b n", p=P)
+    x_view, weight_view, y_view = [m.rearrange("(b p) k -> p b k", p=P) for m in (x, weight, y)]
 
     with ExitStack() as ctx:
         consts = ctx.enter_context(tc.tile_pool(name="consts", bufs=1))
         stage = ctx.enter_context(tc.tile_pool(name="stage", bufs=PREFETCH))
         order_pool = ctx.enter_context(tc.tile_pool(name="ordered", bufs=3))
-        group_pool = ctx.enter_context(tc.tile_pool(name="grouped", bufs=3))
-        code_pool = ctx.enter_context(tc.tile_pool(name="codes", bufs=LAG + 2))
-        last_pool = ctx.enter_context(tc.tile_pool(name="last", bufs=LAST))
+        group_pool = ctx.enter_context(tc.tile_pool(name="grouped", bufs=4))
+        weight_pool = ctx.enter_context(tc.tile_pool(name="weight_codes", bufs=4))
+        x_pool = ctx.enter_context(tc.tile_pool(name="x_codes", bufs=3))
         result_pool = ctx.enter_context(tc.tile_pool(name="result", bufs=BLOCKS))
         turn_psum = ctx.enter_context(tc.psum_pool(name="turn", bufs=TURN_BANKS))
         acc_psum = ctx.enter_context(tc.psum_pool(name="acc", bufs=1))
@@ -66,37 +61,40 @@ def tile_modelnew_k_kernel(
         staged = {}
         odd_run = {}
 
-        def pieces(c):
-            return [slice(0, 2), slice(2, 4)] if c == 0 else [slice(0, BLOCKS)]
-
-        def load_chunk(c):
-            k0, width = sum(widths[:c]), widths[c]
-            for operand in range(2):
-                tile = stage.tile([P, BLOCKS * width], BF16, tag="staged%d" % operand, name="staged")
-                for blocks in pieces(c):
-                    nc.sync.dma_start(
-                        out=tile[:].rearrange("p (b k) -> p b k", b=BLOCKS)[:, blocks],
-                        in_=views[operand][:, blocks, k0 : k0 + width],
-                    )
-                staged[c, operand] = tile
-
-        def load_vector(vector, name):
-            column = consts.tile([P, PER_PARTITION], BF16, name=name)
-            nc.gpsimd.dma_start(out=column[:], in_=vector.rearrange("(p j) -> p j", j=PER_PARTITION))
-            return column
+        def load_piece(r):
+            chunk, part = divmod(r, PIECES)
+            view = weight_view if part < 2 else x_view
+            b0 = PIECE_BLOCKS * (part % 2)
+            tile = stage.tile([P, PIECE_BLOCKS * CHUNK], BF16, tag="staged", name="staged")
+            step = 1 if r == 0 else PIECE_BLOCKS
+            for b in range(0, PIECE_BLOCKS, step):
+                nc.sync.dma_start(
+                    out=tile[:].rearrange("p (b k) -> p b k", b=PIECE_BLOCKS)[:, b : b + step],
+                    in_=view[:, b0 + b : b0 + b + step, chunk * CHUNK : (chunk + 1) * CHUNK],
+                )
+            staged[r] = tile
 
         ident = consts.tile([P, P], F32)
         make_identity(nc, ident[:])
+        for r in range(VECTORS_BEHIND):
+            load_piece(r)
+
+        def load_vector(vector, name):
+            column = consts.tile([P, PER_PARTITION], BF16, name=name)
+            nc.sync.dma_start(out=column[:], in_=vector.rearrange("(p j) -> p j", j=PER_PARTITION))
+            return column
+
         var_col = load_vector(running_var, "var_col")
         gain_col = load_vector(norm_weight, "gain_col")
         bias_col = load_vector(bias, "bias_col")
         mean_col = load_vector(running_mean, "mean_col")
         offset_col = load_vector(norm_bias, "offset_col")
 
-        for c in range(PREFETCH):
-            load_chunk(c)
         y_sb = consts.tile([P, BLOCKS * FEATURES], BF16)
         nc.sync.dma_start(out=y_sb[:].rearrange("p (b n) -> p b n", b=BLOCKS), in_=y_view)
+
+        for r in range(VECTORS_BEHIND, PREFETCH):
+            load_piece(r)
 
         scale_col = consts.tile([P, PER_PARTITION], F32)
         shift_col = consts.tile([P, PER_PARTITION], F32)
@@ -142,49 +140,43 @@ def tile_modelnew_k_kernel(
                 nc.vector.tensor_mul(out=addend[:, cols], in0=addend[:, cols], in1=y_sb[:, cols])
 
         steps = [(b, step) for b in range(BLOCKS) for step in range(3)]
-        prepare_in_pass = {COLUMNS_FROM + 2 + n: bs for n, bs in enumerate(steps)}
-        assert COLUMNS_FROM >= sum(widths[:PREFETCH]) // K_PASS
+        prepare_in_round = {COLUMNS_FROM + 2 + n: bs for n, bs in enumerate(steps)}
 
-        def half_blocks(c, operand):
-            return staged[c, operand][:].rearrange(
+        def put_in_order(r):
+            tile = order_pool.tile([P, PIECE_BLOCKS * CHUNK // 2], BF16, tag="odd", name="odd_run")
+            odd = tile[:].rearrange("p (m s run e) -> p m s run e", s=RUN // HALF // 2, run=2, e=HALF)
+            halves = staged[r][:].rearrange(
                 "p (m run s par e) -> p m run s par e", run=2, s=RUN // HALF // 2, par=2, e=HALF
             )
-
-        def put_in_order(c, operand):
-            tile = order_pool.tile([P, BLOCKS * widths[c] // 2], BF16, tag="odd%d" % operand, name="odd_run")
-            odd = tile[:].rearrange("p (m s run e) -> p m s run e", s=RUN // HALF // 2, run=2, e=HALF)
-            halves = half_blocks(c, operand)
-            for blocks in pieces(c):
-                passes = widths[c] // K_PASS
-                m = slice(blocks.start * passes, blocks.stop * passes)
+            step = CHUNK_PASSES if r == 0 else SETS
+            for m0 in range(0, SETS, step):
+                m = slice(m0, m0 + step)
                 nc.vector.tensor_copy(
                     out=odd[:, m], in_=halves[:, m, :, :, 1].rearrange("p m run s e -> p m s run e")
                 )
                 nc.vector.tensor_copy(out=halves[:, m, 0, :, 1], in_=halves[:, m, 1, :, 0])
-            odd_run[c, operand] = tile
+            odd_run[r] = tile
 
-        def turn(first, second, grouped, place, copy=nc.scalar.copy):
+        def turn(r, sets, grouped, place):
             bank = turn_psum.tile([P, BANK], F32, tag="bank", name="bank")
-            for h, (g, operand, b) in enumerate((first, second)):
-                c, i = home[g]
-                m = b * (widths[c] // K_PASS) + i
-                for u, (tile, w0) in enumerate(((staged[c, operand], 2 * m * P), (odd_run[c, operand], m * P))):
+            for h, m in enumerate(sets):
+                for u, (tile, w0) in enumerate(((staged[r], 2 * m * P), (odd_run[r], m * P))):
                     words = tile[:].bitcast(F32)
                     q = 2 * h + u
                     nc.tensor.transpose(bank[:, q * P : (q + 1) * P], words[:, w0 : w0 + P], ident[:])
-            copy(
+            nc.scalar.copy(
                 out=grouped[:]
                 .bitcast(F32)[:, place * BANK : (place + 1) * BANK]
                 .rearrange("p (h r u) -> p h r u", h=2, u=2),
                 in_=bank[:].rearrange("p (h u r) -> p h r u", h=2, u=2),
             )
 
-        def group_tile(columns):
-            return group_pool.tile([P, columns * PACK], BF16, align_bytes=64, tag="grouped", name="grouped")
+        def group_tile():
+            return group_pool.tile([P, WIDE * PACK], BF16, align_bytes=64, tag="grouped", name="grouped")
 
-        def quantise(pool, grouped, columns):
-            words = pool.tile([P, columns], U32, align_bytes=64, tag="words", name="words")
-            scales = pool.tile([P, columns], U8, align_bytes=64, tag="scales", name="scales")
+        def quantise(pool, grouped):
+            words = pool.tile([P, WIDE], U32, align_bytes=64, tag="words", name="words")
+            scales = pool.tile([P, WIDE], U8, align_bytes=64, tag="scales", name="scales")
             nc.vector.quantize_mx(out=words[:].bitcast(FP8X4), scales=scales[:], in_=grouped[:])
             return words, scales
 
@@ -192,72 +184,51 @@ def tile_modelnew_k_kernel(
         for b in range(BLOCKS):
             acc.append(acc_psum.tile([P, FEATURES], F32, tag="acc%d" % b, name="acc%d" % b))
 
-        def multiply(g, b, left, l0, right, r0):
-            nc.tensor.matmul_mx(
-                out=acc[b][:],
-                lhsT=left[0][:, l0 : l0 + P].bitcast(FP8X4),
-                lhsT_scale=left[1][:, l0 : l0 + P],
-                rhs=right[0][:, r0 : r0 + FEATURES].bitcast(FP8X4),
-                rhs_scale=right[1][:, r0 : r0 + FEATURES],
-                start=(g == 0),
-                stop=(g == PASSES - 1),
-            )
+        weight_grouped, weight_codes = {}, {}
+        x_grouped, x_codes = {}, {}
 
-        grouped = {}
-        quantised = {}
+        def turn_piece(r):
+            chunk, part = divmod(r, PIECES)
+            h = part % 2
+            if part == 0:
+                for q in range(2):
+                    weight_grouped[chunk, q] = group_tile()
+            if part < 2:
+                for i in range(CHUNK_PASSES):
+                    turn(r, (i, CHUNK_PASSES + i), weight_grouped[chunk, i // 2], 2 * (i % 2) + h)
+            else:
+                x_grouped[chunk, h] = group_tile()
+                for j in range(SETS // 2):
+                    turn(r, (2 * j, 2 * j + 1), x_grouped[chunk, h], j)
 
-        def multiply_pass(g):
-            for b in range(BLOCKS):
-                multiply(g, b, quantised[g], b * P, quantised[g], ROWS)
+        def quantise_weight(chunk, h):
+            weight_codes[chunk, h] = quantise(weight_pool, weight_grouped[chunk, h])
 
-        for operand in range(2):
-            put_in_order(0, operand)
-        first_last = PASSES - LAST
-        for g in range(first_last):
-            grouped[g] = group_tile(ROWS + FEATURES)
-            for j in range(TURN_BANKS):
-                b = 2 * (j % 2)
-                turn((g, j // 2, b), (g, j // 2, b + 1), grouped[g], j)
-            c, i = home[g]
-            passes = widths[c] // K_PASS
-            next_operands = [operand for operand in range(2) if operand * passes // 2 == i]
-            for operand in next_operands:
-                put_in_order(c + 1, operand)
-            if g >= 1:
-                quantised[g - 1] = quantise(code_pool, grouped[g - 1], ROWS + FEATURES)
-            if i == passes - 1 and c + PREFETCH < len(widths):
-                load_chunk(c + PREFETCH)
-            if g in prepare_in_pass:
-                prepare(*prepare_in_pass[g])
-            if g == COLUMNS_FROM:
-                finish_columns()
-            if g == COLUMNS_FROM + 1:
-                spread_over_partitions(scale_col, scale_bc)
-                spread_over_partitions(shift_col, shift_bc)
-            if g >= LAG:
-                multiply_pass(g - LAG)
+        def quantise_x(chunk, h):
+            x_codes[chunk, h] = quantise(x_pool, x_grouped[chunk, h])
 
-        last_passes = range(first_last, PASSES)
-        weight_codes = {}
-        x_codes = {}
+        def quantise_in_round(r):
+            chunk, part = divmod(r, PIECES)
+            if part >= 2:
+                quantise_weight(chunk, part - 2)
+            elif chunk >= 1:
+                quantise_x(chunk - 1, part)
 
-        def last_weight(g):
-            tile = group_tile(FEATURES)
-            for place in range(2):
-                copy = nc.vector.tensor_copy if place == 1 and g == PASSES - 1 else nc.scalar.copy
-                turn((g, 1, 2 * place), (g, 1, 2 * place + 1), tile, place, copy)
-            return tile
-
-        def last_x(b):
-            tile = group_tile(LAST * P)
-            for place in range(LAST // 2):
-                g = first_last + 2 * place
-                turn((g, 0, b), (g + 1, 0, b), tile, place)
-            return tile
-
-        def multiply_row_block(b):
-            for n, g in enumerate(last_passes):
-                multiply(g, b, x_codes[b], n * P, weight_codes[g], 0)
+        def multiply(n):
+            chunk, b = divmod(n, BLOCKS)
+            for i in range(CHUNK_PASSES):
+                g = CHUNK_PASSES * chunk + i
+                left, l0 = x_codes[chunk, b // 2], ((b % 2) * CHUNK_PASSES + i) * P
+                right, r0 = weight_codes[chunk, i // 2], (i % 2) * FEATURES
+                nc.tensor.matmul_mx(
+                    out=acc[b][:],
+                    lhsT=left[0][:, l0 : l0 + P].bitcast(FP8X4),
+                    lhsT_scale=left[1][:, l0 : l0 + P],
+                    rhs=right[0][:, r0 : r0 + FEATURES].bitcast(FP8X4),
+                    rhs_scale=right[1][:, r0 : r0 + FEATURES],
+                    start=(g == 0),
+                    stop=(g == PASSES - 1),
+                )
 
         def finish_row_block(b):
             result = result_pool.tile([P, FEATURES], F32, tag="result", name="result")
@@ -274,26 +245,29 @@ def tile_modelnew_k_kernel(
                 )
                 nc.sync.dma_start(out=out[b * P : (b + 1) * P, n : n + width], in_=result[:, n : n + width])
 
-        tiles = {}
-        for g in last_passes:
-            tiles[g] = last_weight(g)
-            if g == first_last:
-                c = home[g][0]
-                put_in_order(c + 1, 1)
-                quantised[g - 1] = quantise(code_pool, grouped[g - 1], ROWS + FEATURES)
-            else:
-                weight_codes[g - 1] = quantise(last_pool, tiles[g - 1], FEATURES)
-            if g == first_last + 1:
-                multiply_pass(first_last - LAG)
-                put_in_order(c + 1, 0)
-        x_tile = last_x(0)
-        weight_codes[PASSES - 1] = quantise(last_pool, tiles[PASSES - 1], FEATURES)
-        multiply_pass(first_last - 1)
-        for b in range(BLOCKS):
-            x_codes[b] = quantise(code_pool, x_tile, LAST * P)
-            if b >= 1:
-                finish_row_block(b - 1)
-            if b + 1 < BLOCKS:
-                x_tile = last_x(b + 1)
-            multiply_row_block(b)
-        finish_row_block(BLOCKS - 1)
+        put_in_order(0)
+        for r in range(ROUNDS):
+            turn_piece(r)
+            if r + 1 < ROUNDS:
+                put_in_order(r + 1)
+            quantise_in_round(r)
+            if r + PREFETCH < ROUNDS:
+                load_piece(r + PREFETCH)
+            if r in prepare_in_round:
+                prepare(*prepare_in_round[r])
+            if r == COLUMNS_FROM:
+                finish_columns()
+            if r == COLUMNS_FROM + 1:
+                spread_over_partitions(scale_col, scale_bc)
+                spread_over_partitions(shift_col, shift_bc)
+            if r >= LAG:
+                multiply(r - LAG)
+
+        last_chunk = PASSES // CHUNK_PASSES - 1
+        for h in range(2):
+            quantise_x(last_chunk, h)
+        for n in range(ROUNDS - LAG, ROUNDS):
+            multiply(n)
+            chunk, b = divmod(n, BLOCKS)
+            if chunk == last_chunk:
+                finish_row_block(b)

@@ -24,18 +24,14 @@ BLOCKS = ROWS // P
 PASSES = K // K_PASS
 PER_PARTITION = FEATURES // P
 
-CHUNK_PASSES = 4
-CHUNK = CHUNK_PASSES * K_PASS
-PIECE_BLOCKS = 2
-SETS = PIECE_BLOCKS * CHUNK_PASSES
-PIECES = 4
-ROUNDS = PASSES // CHUNK_PASSES * PIECES
+SETS = 8
+CHUNKS = [2, 2] + [4] * 7
 WIDE = SETS * P
-LAG = PIECES + 1
-PREFETCH = 12
-VECTORS_BEHIND = 8
-COLUMNS_FROM = VECTORS_BEHIND + 2
 TURN_BANKS = 4
+RUN_BANKS = TURN_BANKS
+PREFETCH = 12
+VECTORS_BEHIND = 16
+COLUMNS_FROM = 16
 
 FLOPS = 2 * ROWS * FEATURES * K
 
@@ -58,54 +54,64 @@ def tile_modelnew_k_kernel(
         acc_psum = ctx.enter_context(tc.psum_pool(name="acc", bufs=1))
         ctx.enter_context(tc.manual_schedule())
 
+        pieces = []
+        blocks_of = [SETS // passes for passes in CHUNKS]
+        for chunk, blocks in enumerate(blocks_of):
+            for view in (weight_view, x_view):
+                pieces += [(chunk, view, b0) for b0 in range(0, BLOCKS, blocks)]
+        assert sum(CHUNKS) == PASSES
+        rounds = len(pieces)
+
         staged = {}
         odd_run = {}
 
         def load_piece(r):
-            chunk, part = divmod(r, PIECES)
-            view = weight_view if part < 2 else x_view
-            b0 = PIECE_BLOCKS * (part % 2)
-            tile = stage.tile([P, PIECE_BLOCKS * CHUNK], BF16, tag="staged", name="staged")
-            step = 1 if r == 0 else PIECE_BLOCKS
-            for b in range(0, PIECE_BLOCKS, step):
+            chunk, view, b0 = pieces[r]
+            blocks = blocks_of[chunk]
+            k0, width = sum(CHUNKS[:chunk]) * K_PASS, CHUNKS[chunk] * K_PASS
+            tile = stage.tile([P, SETS * K_PASS], BF16, tag="staged", name="staged")
+            step = blocks // 2 if r == 0 else blocks
+            for b in range(0, blocks, step):
                 nc.sync.dma_start(
-                    out=tile[:].rearrange("p (b k) -> p b k", b=PIECE_BLOCKS)[:, b : b + step],
-                    in_=view[:, b0 + b : b0 + b + step, chunk * CHUNK : (chunk + 1) * CHUNK],
+                    out=tile[:].rearrange("p (b k) -> p b k", b=blocks)[:, b : b + step],
+                    in_=view[:, b0 + b : b0 + b + step, k0 : k0 + width],
                 )
             staged[r] = tile
 
         ident = consts.tile([P, P], F32)
         make_identity(nc, ident[:])
-        for r in range(VECTORS_BEHIND):
+        for r in range(PREFETCH):
             load_piece(r)
 
-        def load_vector(vector, name):
-            column = consts.tile([P, PER_PARTITION], BF16, name=name)
-            nc.sync.dma_start(out=column[:], in_=vector.rearrange("(p j) -> p j", j=PER_PARTITION))
-            return column
-
-        var_col = load_vector(running_var, "var_col")
-        gain_col = load_vector(norm_weight, "gain_col")
-        bias_col = load_vector(bias, "bias_col")
-        mean_col = load_vector(running_mean, "mean_col")
-        offset_col = load_vector(norm_bias, "offset_col")
-
+        vectors = []
+        for name, vector in (
+            ("var_col", running_var),
+            ("gain_col", norm_weight),
+            ("bias_col", bias),
+            ("mean_col", running_mean),
+            ("offset_col", norm_bias),
+        ):
+            vectors.append((consts.tile([P, PER_PARTITION], BF16, name=name), vector))
+        var_col, gain_col, bias_col, mean_col, offset_col = [column for column, vector in vectors]
         y_sb = consts.tile([P, BLOCKS * FEATURES], BF16)
-        nc.sync.dma_start(out=y_sb[:].rearrange("p (b n) -> p b n", b=BLOCKS), in_=y_view)
 
-        for r in range(VECTORS_BEHIND, PREFETCH):
-            load_piece(r)
+        def load_vectors_and_y():
+            for column, vector in vectors:
+                nc.sync.dma_start(out=column[:], in_=vector.rearrange("(p j) -> p j", j=PER_PARTITION))
+            nc.sync.dma_start(out=y_sb[:].rearrange("p (b n) -> p b n", b=BLOCKS), in_=y_view)
 
         scale_col = consts.tile([P, PER_PARTITION], F32)
         shift_col = consts.tile([P, PER_PARTITION], F32)
         exponent = consts.tile([P, PER_PARTITION], F32)
-        nc.gpsimd.memset(exponent[:], -0.5)
-        nc.gpsimd.tensor_scalar(
-            out=scale_col[:], in0=var_col[:], scalar1=EPS, scalar2=None, op0=mybir.AluOpType.add
-        )
-        nc.gpsimd.tensor_tensor(
-            out=scale_col[:], in0=scale_col[:], in1=exponent[:], op=mybir.AluOpType.pow
-        )
+
+        def begin_columns():
+            nc.gpsimd.memset(exponent[:], -0.5)
+            nc.gpsimd.tensor_scalar(
+                out=scale_col[:], in0=var_col[:], scalar1=EPS, scalar2=None, op0=mybir.AluOpType.add
+            )
+            nc.gpsimd.tensor_tensor(
+                out=scale_col[:], in0=scale_col[:], in1=exponent[:], op=mybir.AluOpType.pow
+            )
 
         def finish_columns():
             nc.vector.tensor_mul(out=scale_col[:], in0=scale_col[:], in1=gain_col[:])
@@ -143,12 +149,12 @@ def tile_modelnew_k_kernel(
         prepare_in_round = {COLUMNS_FROM + 2 + n: bs for n, bs in enumerate(steps)}
 
         def put_in_order(r):
-            tile = order_pool.tile([P, PIECE_BLOCKS * CHUNK // 2], BF16, tag="odd", name="odd_run")
+            tile = order_pool.tile([P, SETS * K_PASS // 2], BF16, tag="odd", name="odd_run")
             odd = tile[:].rearrange("p (m s run e) -> p m s run e", s=RUN // HALF // 2, run=2, e=HALF)
             halves = staged[r][:].rearrange(
                 "p (m run s par e) -> p m run s par e", run=2, s=RUN // HALF // 2, par=2, e=HALF
             )
-            step = CHUNK_PASSES if r == 0 else SETS
+            step = SETS // 2 if r == 0 else SETS
             for m0 in range(0, SETS, step):
                 m = slice(m0, m0 + step)
                 nc.vector.tensor_copy(
@@ -186,49 +192,66 @@ def tile_modelnew_k_kernel(
 
         weight_grouped, weight_codes = {}, {}
         x_grouped, x_codes = {}, {}
+        calls, called = [], []
 
-        def turn_piece(r):
-            chunk, part = divmod(r, PIECES)
-            h = part % 2
-            if part == 0:
-                for q in range(2):
-                    weight_grouped[chunk, q] = group_tile()
-            if part < 2:
-                for i in range(CHUNK_PASSES):
-                    turn(r, (i, CHUNK_PASSES + i), weight_grouped[chunk, i // 2], 2 * (i % 2) + h)
-            else:
-                x_grouped[chunk, h] = group_tile()
+        def banks_of(r):
+            banks = []
+            chunk, view, b0 = pieces[r]
+            passes, blocks = CHUNKS[chunk], blocks_of[chunk]
+            if view is x_view:
+                x_grouped[chunk, b0] = group_tile()
                 for j in range(SETS // 2):
-                    turn(r, (2 * j, 2 * j + 1), x_grouped[chunk, h], j)
+                    banks.append((r, (2 * j, 2 * j + 1), x_grouped[chunk, b0], j))
+                calls.append((r, x_grouped, x_codes, x_pool, (chunk, b0)))
+            else:
+                if b0 == 0:
+                    for q in range(passes // 2):
+                        weight_grouped[chunk, q] = group_tile()
+                for b in range(0, blocks, 2):
+                    for i in range(passes):
+                        sets = (b * passes + i, (b + 1) * passes + i)
+                        banks.append((r, sets, weight_grouped[chunk, i // 2], 2 * (i % 2) + (b0 + b) // 2))
+                if b0 + blocks == BLOCKS:
+                    for q in range(passes // 2):
+                        calls.append((r, weight_grouped, weight_codes, weight_pool, (chunk, q)))
+            return banks
 
-        def quantise_weight(chunk, h):
-            weight_codes[chunk, h] = quantise(weight_pool, weight_grouped[chunk, h])
+        def quantise_next(r):
+            complete, source, target, pool, key = calls[len(called)]
+            target[key] = (r,) + quantise(pool, source[key])
+            called.append(key)
 
-        def quantise_x(chunk, h):
-            x_codes[chunk, h] = quantise(x_pool, x_grouped[chunk, h])
+        products, multiplied = [], []
+        for chunk, passes in enumerate(CHUNKS):
+            products += [(chunk, b, i) for b in range(BLOCKS) for i in range(passes)]
 
-        def quantise_in_round(r):
-            chunk, part = divmod(r, PIECES)
-            if part >= 2:
-                quantise_weight(chunk, part - 2)
-            elif chunk >= 1:
-                quantise_x(chunk - 1, part)
+        def operands(chunk, b, i):
+            b_in_piece = b % blocks_of[chunk]
+            left, l0 = x_codes.get((chunk, b - b_in_piece)), (b_in_piece * CHUNKS[chunk] + i) * P
+            right, r0 = weight_codes.get((chunk, i // 2)), (i % 2) * FEATURES
+            return left, l0, right, r0
 
-        def multiply(n):
-            chunk, b = divmod(n, BLOCKS)
-            for i in range(CHUNK_PASSES):
-                g = CHUNK_PASSES * chunk + i
-                left, l0 = x_codes[chunk, b // 2], ((b % 2) * CHUNK_PASSES + i) * P
-                right, r0 = weight_codes[chunk, i // 2], (i % 2) * FEATURES
-                nc.tensor.matmul_mx(
-                    out=acc[b][:],
-                    lhsT=left[0][:, l0 : l0 + P].bitcast(FP8X4),
-                    lhsT_scale=left[1][:, l0 : l0 + P],
-                    rhs=right[0][:, r0 : r0 + FEATURES].bitcast(FP8X4),
-                    rhs_scale=right[1][:, r0 : r0 + FEATURES],
-                    start=(g == 0),
-                    stop=(g == PASSES - 1),
-                )
+        def multiply_next():
+            chunk, b, i = products[len(multiplied)]
+            multiplied.append((chunk, b, i))
+            g = sum(CHUNKS[:chunk]) + i
+            left, l0, right, r0 = operands(chunk, b, i)
+            nc.tensor.matmul_mx(
+                out=acc[b][:],
+                lhsT=left[1][:, l0 : l0 + P].bitcast(FP8X4),
+                lhsT_scale=left[2][:, l0 : l0 + P],
+                rhs=right[1][:, r0 : r0 + FEATURES].bitcast(FP8X4),
+                rhs_scale=right[2][:, r0 : r0 + FEATURES],
+                start=(g == 0),
+                stop=(g == PASSES - 1),
+            )
+
+        def multiply_run(r):
+            for product in products[len(multiplied) : len(multiplied) + RUN_BANKS]:
+                left, l0, right, r0 = operands(*product)
+                if left is None or right is None or max(left[0], right[0]) >= r:
+                    return
+                multiply_next()
 
         def finish_row_block(b):
             result = result_pool.tile([P, FEATURES], F32, tag="result", name="result")
@@ -245,13 +268,23 @@ def tile_modelnew_k_kernel(
                 )
                 nc.sync.dma_start(out=out[b * P : (b + 1) * P, n : n + width], in_=result[:, n : n + width])
 
-        put_in_order(0)
-        for r in range(ROUNDS):
-            turn_piece(r)
-            if r + 1 < ROUNDS:
-                put_in_order(r + 1)
-            quantise_in_round(r)
-            if r + PREFETCH < ROUNDS:
+        for r in range(2):
+            put_in_order(r)
+        filled = 0
+        for r in range(rounds):
+            for bank in banks_of(r):
+                turn(*bank)
+                filled += 1
+                if filled % RUN_BANKS == 0:
+                    multiply_run(r)
+            if len(called) < len(calls) and calls[len(called)][0] < r:
+                quantise_next(r)
+            if r + 2 < rounds:
+                put_in_order(r + 2)
+            if r + PREFETCH == VECTORS_BEHIND:
+                load_vectors_and_y()
+                begin_columns()
+            if r + PREFETCH < rounds:
                 load_piece(r + PREFETCH)
             if r in prepare_in_round:
                 prepare(*prepare_in_round[r])
@@ -260,14 +293,10 @@ def tile_modelnew_k_kernel(
             if r == COLUMNS_FROM + 1:
                 spread_over_partitions(scale_col, scale_bc)
                 spread_over_partitions(shift_col, shift_bc)
-            if r >= LAG:
-                multiply(r - LAG)
 
-        last_chunk = PASSES // CHUNK_PASSES - 1
-        for h in range(2):
-            quantise_x(last_chunk, h)
-        for n in range(ROUNDS - LAG, ROUNDS):
-            multiply(n)
-            chunk, b = divmod(n, BLOCKS)
-            if chunk == last_chunk:
+        for n in range(len(called), len(calls)):
+            quantise_next(rounds)
+        for chunk, b, i in products[len(multiplied) :]:
+            multiply_next()
+            if sum(CHUNKS[:chunk]) + i == PASSES - 1:
                 finish_row_block(b)

@@ -29,6 +29,7 @@ CHUNKS = [2, 2] + [4] * 7
 WIDE = SETS * P
 TURN_BANKS = 4
 RUN_BANKS = TURN_BANKS
+WARM_UP = 6
 PREFETCH = 12
 VECTORS_BEHIND = 16
 COLUMNS_FROM = 16
@@ -246,10 +247,19 @@ def tile_modelnew_k_kernel(
                 stop=(g == PASSES - 1),
             )
 
+        zeros = consts.tile([P, BANK], BF16)
+        nc.vector.memset(zeros[:], 0.0)
+
+        def multiply_zeros(count):
+            bank = turn_psum.tile([P, BANK], F32, tag="bank", name="bank")
+            for n in range(count):
+                nc.tensor.matmul(bank[:], lhsT=zeros[:, :P], rhs=zeros[:], start=True, stop=True)
+
         def multiply_run(r):
-            for product in products[len(multiplied) : len(multiplied) + RUN_BANKS]:
+            for n, product in enumerate(products[len(multiplied) : len(multiplied) + RUN_BANKS]):
                 left, l0, right, r0 = operands(*product)
                 if left is None or right is None or max(left[0], right[0]) >= r:
+                    multiply_zeros(RUN_BANKS - n)
                     return
                 multiply_next()
 
@@ -268,6 +278,7 @@ def tile_modelnew_k_kernel(
                 )
                 nc.sync.dma_start(out=out[b * P : (b + 1) * P, n : n + width], in_=result[:, n : n + width])
 
+        multiply_zeros(WARM_UP)
         for r in range(2):
             put_in_order(r)
         filled = 0

from contextlib import ExitStack

import concourse.mybir as mybir
from concourse.masks import make_identity

F32 = mybir.dt.float32
BF16 = mybir.dt.bfloat16
U32 = mybir.dt.uint32
U8 = mybir.dt.uint8
FP8X4 = mybir.dt.float8_e4m3fn_x4

P = 128
PACK = 4
K_PASS = P * PACK
BANK = 512
HALF = 16
RUN = 256

ROWS = 512
FEATURES = 512
K = 16384
EPS = 1e-5
BLOCKS = ROWS // P
PASSES = K // K_PASS
PER_PARTITION = FEATURES // P

SETS = 8
CHUNKS = [2, 2] + [4] * 7
WIDE = SETS * P
TURN_BANKS = 4
RUN_BANKS = TURN_BANKS
WARM_UP = 6
PREFETCH = 12
VECTORS_BEHIND = 16
COLUMNS_FROM = 16

FLOPS = 2 * ROWS * FEATURES * K


def tile_modelnew_k_kernel(
    tc, x, y, weight, bias, running_mean, running_var, norm_weight, norm_bias, out
):
    nc = tc.nc
    x_view, weight_view, y_view = [m.rearrange("(b p) k -> p b k", p=P) for m in (x, weight, y)]

    with ExitStack() as ctx:
        consts = ctx.enter_context(tc.tile_pool(name="consts", bufs=1))
        stage = ctx.enter_context(tc.tile_pool(name="stage", bufs=PREFETCH))
        order_pool = ctx.enter_context(tc.tile_pool(name="ordered", bufs=3))
        group_pool = ctx.enter_context(tc.tile_pool(name="grouped", bufs=4))
        weight_pool = ctx.enter_context(tc.tile_pool(name="weight_codes", bufs=4))
        x_pool = ctx.enter_context(tc.tile_pool(name="x_codes", bufs=3))
        result_pool = ctx.enter_context(tc.tile_pool(name="result", bufs=BLOCKS))
        turn_psum = ctx.enter_context(tc.psum_pool(name="turn", bufs=TURN_BANKS))
        acc_psum = ctx.enter_context(tc.psum_pool(name="acc", bufs=1))
        ctx.enter_context(tc.manual_schedule())

        pieces = []
        blocks_of = [SETS // passes for passes in CHUNKS]
        for chunk, blocks in enumerate(blocks_of):
            for view in (weight_view, x_view):
                pieces += [(chunk, view, b0) for b0 in range(0, BLOCKS, blocks)]
        assert sum(CHUNKS) == PASSES
        rounds = len(pieces)

        staged = {}
        odd_run = {}

        def load_piece(r):
            chunk, view, b0 = pieces[r]
            blocks = blocks_of[chunk]
            k0, width = sum(CHUNKS[:chunk]) * K_PASS, CHUNKS[chunk] * K_PASS
            tile = stage.tile([P, SETS * K_PASS], BF16, tag="staged", name="staged")
            step = blocks // 2 if r == 0 else blocks
            for b in range(0, blocks, step):
                nc.sync.dma_start(
                    out=tile[:].rearrange("p (b k) -> p b k", b=blocks)[:, b : b + step],
                    in_=view[:, b0 + b : b0 + b + step, k0 : k0 + width],
                )
            staged[r] = tile

        ident = consts.tile([P, P], F32)
        make_identity(nc, ident[:])
        for r in range(PREFETCH):
            load_piece(r)

        vectors = []
        for name, vector in (
            ("var_col", running_var),
            ("gain_col", norm_weight),
            ("bias_col", bias),
            ("mean_col", running_mean),
            ("offset_col", norm_bias),
        ):
            vectors.append((consts.tile([P, PER_PARTITION], BF16, name=name), vector))
        var_col, gain_col, bias_col, mean_col, offset_col = [column for column, vector in vectors]
        y_sb = consts.tile([P, BLOCKS * FEATURES], BF16)

        def load_vectors_and_y():
            for column, vector in vectors:
                nc.sync.dma_start(out=column[:], in_=vector.rearrange("(p j) -> p j", j=PER_PARTITION))
            nc.sync.dma_start(out=y_sb[:].rearrange("p (b n) -> p b n", b=BLOCKS), in_=y_view)

        scale_col = consts.tile([P, PER_PARTITION], F32)
        shift_col = consts.tile([P, PER_PARTITION], F32)
        exponent = consts.tile([P, PER_PARTITION], F32)

        def begin_columns():
            nc.gpsimd.memset(exponent[:], -0.5)
            nc.gpsimd.tensor_scalar(
                out=scale_col[:], in0=var_col[:], scalar1=EPS, scalar2=None, op0=mybir.AluOpType.add
            )
            nc.gpsimd.tensor_tensor(
                out=scale_col[:], in0=scale_col[:], in1=exponent[:], op=mybir.AluOpType.pow
            )

        def finish_columns():
            nc.vector.tensor_mul(out=scale_col[:], in0=scale_col[:], in1=gain_col[:])
            nc.vector.tensor_sub(out=shift_col[:], in0=bias_col[:], in1=mean_col[:])
            nc.vector.tensor_mul(out=shift_col[:], in0=shift_col[:], in1=scale_col[:])
            nc.vector.tensor_add(out=shift_col[:], in0=shift_col[:], in1=offset_col[:])

        scale_bc = consts.tile([P, FEATURES], F32)
        shift_bc = consts.tile([P, FEATURES], F32)

        def spread_over_partitions(column, row):
            bank = turn_psum.tile([P, BANK], F32, tag="bank", name="bank")
            for j in range(PER_PARTITION):
                nc.tensor.transpose(
                    bank[:, j * P : (j + 1) * P], column[:, j : j + 1].to_broadcast([P, P]), ident[:]
                )
            nc.scalar.copy(
                out=row[:].rearrange("m (p j) -> m p j", j=PER_PARTITION),
                in_=bank[:].rearrange("m (j p) -> m p j", j=PER_PARTITION),
            )

        factor = consts.tile([P, BLOCKS * FEATURES], F32)
        addend = consts.tile([P, BLOCKS * FEATURES], F32)

        def prepare(b, step):
            cols = slice(b * FEATURES, (b + 1) * FEATURES)
            if step == 0:
                nc.vector.tensor_add(out=addend[:, cols], in0=shift_bc[:], in1=y_sb[:, cols])
            elif step == 1:
                nc.vector.tensor_mul(out=factor[:, cols], in0=scale_bc[:], in1=y_sb[:, cols])
            else:
                nc.vector.tensor_mul(out=addend[:, cols], in0=addend[:, cols], in1=y_sb[:, cols])

        steps = [(b, step) for b in range(BLOCKS) for step in range(3)]
        prepare_in_round = {COLUMNS_FROM + 2 + n: bs for n, bs in enumerate(steps)}

        def put_in_order(r):
            tile = order_pool.tile([P, SETS * K_PASS // 2], BF16, tag="odd", name="odd_run")
            odd = tile[:].rearrange("p (m s run e) -> p m s run e", s=RUN // HALF // 2, run=2, e=HALF)
            halves = staged[r][:].rearrange(
                "p (m run s par e) -> p m run s par e", run=2, s=RUN // HALF // 2, par=2, e=HALF
            )
            step = SETS // 2 if r == 0 else SETS
            for m0 in range(0, SETS, step):
                m = slice(m0, m0 + step)
                nc.vector.tensor_copy(
                    out=odd[:, m], in_=halves[:, m, :, :, 1].rearrange("p m run s e -> p m s run e")
                )
                nc.vector.tensor_copy(out=halves[:, m, 0, :, 1], in_=halves[:, m, 1, :, 0])
            odd_run[r] = tile

        def turn(r, sets, grouped, place):
            bank = turn_psum.tile([P, BANK], F32, tag="bank", name="bank")
            for h, m in enumerate(sets):
                for u, (tile, w0) in enumerate(((staged[r], 2 * m * P), (odd_run[r], m * P))):
                    words = tile[:].bitcast(F32)
                    q = 2 * h + u
                    nc.tensor.transpose(bank[:, q * P : (q + 1) * P], words[:, w0 : w0 + P], ident[:])
            nc.scalar.copy(
                out=grouped[:]
                .bitcast(F32)[:, place * BANK : (place + 1) * BANK]
                .rearrange("p (h r u) -> p h r u", h=2, u=2),
                in_=bank[:].rearrange("p (h u r) -> p h r u", h=2, u=2),
            )

        def group_tile():
            return group_pool.tile([P, WIDE * PACK], BF16, align_bytes=64, tag="grouped", name="grouped")

        def quantise(pool, grouped):
            words = pool.tile([P, WIDE], U32, align_bytes=64, tag="words", name="words")
            scales = pool.tile([P, WIDE], U8, align_bytes=64, tag="scales", name="scales")
            nc.vector.quantize_mx(out=words[:].bitcast(FP8X4), scales=scales[:], in_=grouped[:])
            return words, scales

        acc = []
        for b in range(BLOCKS):
            acc.append(acc_psum.tile([P, FEATURES], F32, tag="acc%d" % b, name="acc%d" % b))

        weight_grouped, weight_codes = {}, {}
        x_grouped, x_codes = {}, {}
        calls, called = [], []

        def banks_of(r):
            banks = []
            chunk, view, b0 = pieces[r]
            passes, blocks = CHUNKS[chunk], blocks_of[chunk]
            if view is x_view:
                x_grouped[chunk, b0] = group_tile()
                for j in range(SETS // 2):
                    banks.append((r, (2 * j, 2 * j + 1), x_grouped[chunk, b0], j))
                calls.append((r, x_grouped, x_codes, x_pool, (chunk, b0)))
            else:
                if b0 == 0:
                    for q in range(passes // 2):
                        weight_grouped[chunk, q] = group_tile()
                for b in range(0, blocks, 2):
                    for i in range(passes):
                        sets = (b * passes + i, (b + 1) * passes + i)
                        banks.append((r, sets, weight_grouped[chunk, i // 2], 2 * (i % 2) + (b0 + b) // 2))
                if b0 + blocks == BLOCKS:
                    for q in range(passes // 2):
                        calls.append((r, weight_grouped, weight_codes, weight_pool, (chunk, q)))
            return banks

        def quantise_next(r):
            complete, source, target, pool, key = calls[len(called)]
            target[key] = (r,) + quantise(pool, source[key])
            called.append(key)

        products, multiplied = [], []
        for chunk, passes in enumerate(CHUNKS):
            products += [(chunk, b, i) for b in range(BLOCKS) for i in range(passes)]

        def operands(chunk, b, i):
            b_in_piece = b % blocks_of[chunk]
            left, l0 = x_codes.get((chunk, b - b_in_piece)), (b_in_piece * CHUNKS[chunk] + i) * P
            right, r0 = weight_codes.get((chunk, i // 2)), (i % 2) * FEATURES
            return left, l0, right, r0

        def multiply_next():
            chunk, b, i = products[len(multiplied)]
            multiplied.append((chunk, b, i))
            g = sum(CHUNKS[:chunk]) + i
            left, l0, right, r0 = operands(chunk, b, i)
            nc.tensor.matmul_mx(
                out=acc[b][:],
                lhsT=left[1][:, l0 : l0 + P].bitcast(FP8X4),
                lhsT_scale=left[2][:, l0 : l0 + P],
                rhs=right[1][:, r0 : r0 + FEATURES].bitcast(FP8X4),
                rhs_scale=right[2][:, r0 : r0 + FEATURES],
                start=(g == 0),
                stop=(g == PASSES - 1),
            )

        zeros = consts.tile([P, BANK], BF16)
        nc.vector.memset(zeros[:], 0.0)

        def multiply_zeros(count):
            bank = turn_psum.tile([P, BANK], F32, tag="bank", name="bank")
            for n in range(count):
                nc.tensor.matmul(bank[:], lhsT=zeros[:, :P], rhs=zeros[:], start=True, stop=True)

        def multiply_run(r):
            for n, product in enumerate(products[len(multiplied) : len(multiplied) + RUN_BANKS]):
                left, l0, right, r0 = operands(*product)
                if left is None or right is None or max(left[0], right[0]) >= r:
                    multiply_zeros(RUN_BANKS - n)
                    return
                multiply_next()

        def finish_row_block(b):
            result = result_pool.tile([P, FEATURES], F32, tag="result", name="result")
            width = FEATURES // 2
            for n in range(0, FEATURES, width):
                f0 = b * FEATURES + n
                nc.vector.tensor_mul(
                    out=result[:, n : n + width], in0=acc[b][:, n : n + width], in1=factor[:, f0 : f0 + width]
                )
            for n in range(0, FEATURES, width):
                f0 = b * FEATURES + n
                nc.vector.tensor_add(
                    out=result[:, n : n + width], in0=result[:, n : n + width], in1=addend[:, f0 : f0 + width]
                )
                nc.sync.dma_start(out=out[b * P : (b + 1) * P, n : n + width], in_=result[:, n : n + width])

        multiply_zeros(WARM_UP)
        for r in range(2):
            put_in_order(r)
        filled = 0
        for r in range(rounds):
            for bank in banks_of(r):
                turn(*bank)
                filled += 1
                if filled % RUN_BANKS == 0:
                    multiply_run(r)
            if len(called) < len(calls) and calls[len(called)][0] < r:
                quantise_next(r)
            if r + 2 < rounds:
                put_in_order(r + 2)
            if r + PREFETCH == VECTORS_BEHIND:
                load_vectors_and_y()
                begin_columns()
            if r + PREFETCH < rounds:
                load_piece(r + PREFETCH)
            if r in prepare_in_round:
                prepare(*prepare_in_round[r])
            if r == COLUMNS_FROM:
                finish_columns()
            if r == COLUMNS_FROM + 1:
                spread_over_partitions(scale_col, scale_bc)
                spread_over_partitions(shift_col, shift_bc)

        for n in range(len(called), len(calls)):
            quantise_next(rounds)
        for chunk, b, i in products[len(multiplied) :]:
            multiply_next()
            if sum(CHUNKS[:chunk]) + i == PASSES - 1:
                finish_row_block(b)
